import numpy as np
import ml_dtypes


def mxq(x, axis, fmt="e4m3"):
    dtype, down = {"e4m3": (ml_dtypes.float8_e4m3fn, 7), "e5m2": (ml_dtypes.float8_e5m2, 14)}[fmt]
    v = np.moveaxis(np.asarray(x, np.float32).astype(ml_dtypes.bfloat16).astype(np.float64), axis, -1)
    blocks = v.reshape(v.shape[:-1] + (-1, 32))
    amax = np.abs(blocks).max(-1, keepdims=True)
    byte = np.maximum(np.where(amax > 0, np.frexp(amax)[1] - 1 + 127, 0) - down, 1)
    scale = np.exp2(byte - 127.0)
    codes = (blocks / scale).astype(np.float32).astype(dtype).astype(np.float64)
    return np.moveaxis((codes * scale).reshape(v.shape), -1, axis)


WIDE = False


def mx_kscale(k):
    if not WIDE:
        return np.ones(k)
    levels = np.array([10, -10, 5, -5, 0])
    a = np.random.permutation(np.resize(levels, k // 512 * 4)).reshape(k // 512, 4)
    idx = np.arange(k)
    return np.exp2(a[idx // 512, idx % 128 // 32])


BF16 = ml_dtypes.bfloat16


def bf(x):
    return np.asarray(x, np.float32).astype(BF16)


def f64(x):
    return np.asarray(x).astype(np.float64)


B, R, C, D, S, T, DIL, KT = 2, 512, 512, 512, 128, 128, 64, 2


def sigmoid(v):
    return 1.0 / (1.0 + np.exp(-v))


def setup_inputs():
    s = mx_kscale(C)
    return {
        "x": bf(np.random.standard_normal((B, R, T))),
        "cond": bf(np.random.standard_normal((B, C, T)) * s[None, :, None]),
        "w_sig": bf(np.random.standard_normal((D, R, KT)) * 0.6 / np.sqrt(R)),
        "b_sig": bf(np.random.standard_normal(D) * 0.3),
        "w_gate": bf(np.random.standard_normal((D, R, KT)) * 0.6 / np.sqrt(R)),
        "b_gate": bf(np.random.standard_normal(D) * 0.3),
        "w_psig": bf(np.random.standard_normal((D, C)) * 0.6 / np.sqrt(C) / s[None, :]),
        "w_pgate": bf(np.random.standard_normal((D, C)) * 0.6 / np.sqrt(C) / s[None, :]),
        "w_res": bf(np.random.standard_normal((R, D)) * 2.0 / np.sqrt(D)),
        "w_skp": bf(np.random.standard_normal((S, D)) * 2.0 / np.sqrt(D)),
    }


def reference(x, cond, w_sig, b_sig, w_gate, b_gate, w_psig, w_pgate, w_res, w_skp):
    x = f64(x)
    x1 = x[:, :, DIL:]
    xq = mxq(x, 1, "e4m3")
    x0q = xq[:, :, :-DIL]
    x1q = xq[:, :, DIL:]
    cq = mxq(f64(cond)[:, :, DIL:], 1, "e4m3")
    wsq = mxq(f64(w_sig), 1, "e4m3")
    wgq = mxq(f64(w_gate), 1, "e4m3")
    filt = ((wsq[:, :, 0] @ x0q)
            + (wsq[:, :, 1] @ x1q)
            + (mxq(f64(w_psig), 1, "e4m3") @ cq)
            + f64(b_sig)[None, :, None])
    gate = ((wgq[:, :, 0] @ x0q)
            + (wgq[:, :, 1] @ x1q)
            + (mxq(f64(w_pgate), 1, "e4m3") @ cq)
            + f64(b_gate)[None, :, None])
    z = np.tanh(filt) * sigmoid(gate)
    zq = mxq(z, 1, "e4m3")
    sig = (mxq(f64(w_res), 1, "e4m3") @ zq) + x1
    skp = mxq(f64(w_skp), 1, "e4m3") @ zq
    return (sig, skp)

@@ -1,0 +1,199 @@
+from contextlib import ExitStack
+
+import concourse.mybir as mybir
+from concourse.masks import make_identity
+
+F32 = mybir.dt.float32
+BF16 = mybir.dt.bfloat16
+U32 = mybir.dt.uint32
+U8 = mybir.dt.uint8
+FP8X4 = mybir.dt.float8_e4m3fn_x4
+ACT = mybir.ActivationFunctionType
+ALU = mybir.AluOpType
+
+P = 128
+PACK = 4
+B = 2
+CH = 512
+SKIP = 128
+T = 128
+DIL = 64
+TAPS = 2
+N = B * DIL
+HALVES = 2
+
+FLOPS = 2 * N * (6 * CH * CH + CH * CH + SKIP * CH)
+
+
+def tile_gatedresidualcondconv_pa_s_kernel(
+    tc, x, cond, w_sig, b_sig, w_gate, b_gate, w_psig, w_pgate, w_res, w_skp, out_0, out_1
+):
+    nc = tc.nc
+    with ExitStack() as ctx:
+        const = ctx.enter_context(tc.tile_pool(name="const", bufs=1))
+        raw = ctx.enter_context(tc.tile_pool(name="raw", bufs=1))
+        stage = ctx.enter_context(tc.tile_pool(name="stage", bufs=1))
+        mx = ctx.enter_context(tc.tile_pool(name="mx", bufs=1))
+        turned = ctx.enter_context(tc.psum_pool(name="turned", bufs=6))
+        sums = ctx.enter_context(tc.psum_pool(name="sums", bufs=2))
+
+        ident = const.tile([P, P], F32)
+        make_identity(nc, ident[:])
+        warm = const.tile([P, 1], F32)
+        nc.vector.memset(warm[:], 0.0)
+        nc.scalar.activation(out=warm[:], in_=warm[:], func=ACT.Sigmoid)
+
+        def load(name, shape, view):
+            rows = raw.tile(shape, BF16, name=name)
+            nc.sync.dma_start(out=rows[:], in_=view)
+            return rows
+
+        sig_view = w_sig.rearrange("(u p e) r t -> p u e (r t)", u=HALVES, e=2)
+        gate_view = w_gate.rearrange("(u p e) r t -> p u e (r t)", u=HALVES, e=2)
+        psig_view = w_psig.rearrange("(u p e) c -> p u e c", u=HALVES, e=2)
+        pgate_view = w_pgate.rearrange("(u p e) c -> p u e c", u=HALVES, e=2)
+        res_view = w_res.rearrange("(h i p) d -> p h i d", h=2, i=2)
+
+        sig_rows = [None] * PACK
+        gate_rows = [None] * PACK
+        sig_rows[0] = load("sig0", [P, TAPS * CH], sig_view[:, 0, 0, :])
+        x_sb = load("x_sb", [P, B * PACK, T], x.rearrange("b (j p) t -> p (b j) t", p=P))
+        gate_rows[0] = load("gate0", [P, TAPS * CH], gate_view[:, 0, 0, :])
+        c_sb = load(
+            "c_sb", [P, B * HALVES, 2 * T], cond.rearrange("b (u p e) t -> p (b u) (e t)", u=HALVES, e=2)
+        )
+        sig_rows[1] = load("sig1", [P, TAPS * CH], sig_view[:, 0, 1, :])
+        psig_rows = [load("psig0", [P, 2, CH], psig_view[:, 0])]
+        gate_rows[1] = load("gate1", [P, TAPS * CH], gate_view[:, 0, 1, :])
+        pgate_rows = [load("pgate0", [P, 2, CH], pgate_view[:, 0])]
+        sig_rows[2] = load("sig2", [P, TAPS * CH], sig_view[:, 1, 0, :])
+        psig_rows.append(load("psig1", [P, 2, CH], psig_view[:, 1]))
+        gate_rows[2] = load("gate2", [P, TAPS * CH], gate_view[:, 1, 0, :])
+        pgate_rows.append(load("pgate1", [P, 2, CH], pgate_view[:, 1]))
+        sig_rows[3] = load("sig3", [P, TAPS * CH], sig_view[:, 1, 1, :])
+        res_rows = [load("res0", [P, 2, CH], res_view[:, 0])]
+        gate_rows[3] = load("gate3", [P, TAPS * CH], gate_view[:, 1, 1, :])
+        res_rows.append(load("res1", [P, 2, CH], res_view[:, 1]))
+        skp_rows = load("skp", [P, 1, CH], w_skp.rearrange("s (o d) -> s o d", o=1))
+
+        bias_sig = const.tile([P, PACK], BF16)
+        nc.scalar.dma_start(
+            out=bias_sig[:].rearrange("p (u e) -> p u e", u=HALVES),
+            in_=b_sig.rearrange("(u p e) -> p u e", u=HALVES, e=2),
+        )
+        bias_gate = const.tile([P, PACK], BF16)
+        nc.scalar.dma_start(
+            out=bias_gate[:].rearrange("p (u e) -> p u e", u=HALVES),
+            in_=b_gate.rearrange("(u p e) -> p u e", u=HALVES, e=2),
+        )
+
+        def quantise(name, grouped_flat, columns):
+            codes = mx.tile([P, columns], U32, name=name + "_codes", align_bytes=64)
+            scales = mx.tile([P, columns], U8, name=name + "_scales", align_bytes=64)
+            nc.vector.quantize_mx(out=codes[:].bitcast(FP8X4), scales=scales[:], in_=grouped_flat)
+            return codes, scales
+
+        def tap_weights(name, rows):
+            words = rows[:].bitcast(F32)
+            bank = turned.tile([P, PACK, P], F32, tag="bank", name=name + "_bank")
+            for j in range(PACK):
+                nc.tensor.transpose(bank[:, j, :], words[:, j * P : (j + 1) * P], ident[:])
+            grouped = stage.tile([P, TAPS, P, PACK], BF16, name=name + "_grouped", align_bytes=64)
+            nc.scalar.copy(
+                out=grouped[:], in_=bank[:].bitcast(BF16).rearrange("p j (m t) -> p t m j", t=TAPS)
+            )
+            return quantise(name, grouped[:].rearrange("p t m j -> p (t m j)"), TAPS * P)
+
+        def plain_weights(name, rows, chunks):
+            bank = turned.tile([P, chunks, HALVES, P], F32, tag="bank", name=name + "_bank")
+            for i in range(chunks):
+                words = rows[:, i, :].bitcast(F32)
+                for v in range(HALVES):
+                    nc.tensor.transpose(bank[:, i, v, :], words[:, v * P : (v + 1) * P], ident[:])
+            grouped = stage.tile([P, chunks, P, PACK], BF16, name=name + "_grouped", align_bytes=64)
+            nc.vector.tensor_copy(
+                out=grouped[:].bitcast(F32), in_=bank[:].rearrange("p i v m -> p i m v")
+            )
+            return quantise(name, grouped[:].rearrange("p i m t -> p (i m t)"), chunks * P)
+
+        def mx_pass(out, weights, first, moving, moving_first, start, stop):
+            w_codes, w_scales = weights
+            m_codes, m_scales = moving
+            nc.tensor.matmul_mx(
+                out=out,
+                lhsT=w_codes[:, first : first + P].bitcast(FP8X4),
+                lhsT_scale=w_scales[:, first : first + P],
+                rhs=m_codes[:, moving_first : moving_first + N].bitcast(FP8X4),
+                rhs_scale=m_scales[:, moving_first : moving_first + N],
+                start=start,
+                stop=stop,
+            )
+
+        x_grouped = stage.tile([P, TAPS, B, DIL, PACK], BF16, align_bytes=64)
+        x_by_time = x_sb[:].rearrange("p (b j) t -> p b t j", b=B)
+        for h in range(TAPS):
+            nc.vector.tensor_copy(out=x_grouped[:, h], in_=x_by_time[:, :, h * DIL : (h + 1) * DIL, :])
+        x_mx = quantise("x", x_grouped[:].rearrange("p h b t j -> p (h b t j)"), TAPS * N)
+
+        c_grouped = stage.tile([P, B, DIL, PACK], BF16, align_bytes=64)
+        c_by_time = c_sb[:].rearrange("p (b u) (e t) -> p b t (u e)", b=B, e=2)
+        nc.vector.tensor_copy(out=c_grouped[:], in_=c_by_time[:, :, DIL:T, :])
+        c_mx = quantise("c", c_grouped[:].rearrange("p b t s -> p (b t s)"), N)
+
+        tanh_filt = stage.tile([P, PACK, N], F32)
+        sigm_gate = stage.tile([P, PACK, N], F32)
+        for u in range(HALVES):
+            sig_mx = [None, None]
+            gate_mx = [None, None]
+            for e in range(2):
+                s = 2 * u + e
+                sig_mx[e] = tap_weights("sig%d" % s, sig_rows[s])
+                gate_mx[e] = tap_weights("gate%d" % s, gate_rows[s])
+            psig_mx = plain_weights("psig%d" % u, psig_rows[u], 2)
+            pgate_mx = plain_weights("pgate%d" % u, pgate_rows[u], 2)
+            for e in range(2):
+                s = 2 * u + e
+                acc = sums.tile([P, 2, N], F32, tag="sum", name="acc%d" % s)
+                for g, (taps_mx, proj_mx) in enumerate(((sig_mx[e], psig_mx), (gate_mx[e], pgate_mx))):
+                    mx_pass(acc[:, g, :], taps_mx, 0, x_mx, 0, True, False)
+                    mx_pass(acc[:, g, :], taps_mx, P, x_mx, N, False, False)
+                    mx_pass(acc[:, g, :], proj_mx, e * P, c_mx, 0, False, True)
+                nc.scalar.activation(
+                    out=sigm_gate[:, s, :], in_=acc[:, 1, :], func=ACT.Sigmoid, bias=bias_gate[:, s : s + 1]
+                )
+                nc.scalar.activation(
+                    out=tanh_filt[:, s, :], in_=acc[:, 0, :], func=ACT.Tanh, bias=bias_sig[:, s : s + 1]
+                )
+
+        res_mx = [plain_weights("res%d" % h, res_rows[h], 2) for h in range(2)]
+        skp_mx = plain_weights("skp", skp_rows, 1)
+
+        z_grouped = stage.tile([P, N, PACK], BF16, align_bytes=64)
+        nc.vector.tensor_tensor(
+            out=z_grouped[:],
+            in0=tanh_filt[:].rearrange("p s n -> p n s"),
+            in1=sigm_gate[:].rearrange("p s n -> p n s"),
+            op=ALU.mult,
+        )
+        z_mx = quantise("z", z_grouped[:].rearrange("p n s -> p (n s)"), N)
+
+        res_sum = sums.tile([P, PACK, N], F32, tag="sum")
+        for j in range(PACK):
+            mx_pass(res_sum[:, j, :], res_mx[j // 2], (j % 2) * P, z_mx, 0, True, True)
+        skp_sum = sums.tile([P, N], F32, tag="sum")
+        mx_pass(skp_sum[:], skp_mx, 0, z_mx, 0, True, True)
+
+        sig_sb = stage.tile([P, B, PACK, DIL], F32)
+        nc.vector.tensor_tensor(
+            out=sig_sb[:].rearrange("p b j t -> p j b t"),
+            in0=res_sum[:].rearrange("p j (b t) -> p j b t", b=B),
+            in1=x_sb[:].rearrange("p (b j) t -> p j b t", b=B)[:, :, :, DIL:T],
+            op=ALU.add,
+        )
+        nc.sync.dma_start(
+            out=out_0.rearrange("b (j p) t -> p (b j) t", p=P),
+            in_=sig_sb[:].rearrange("p b j t -> p (b j) t"),
+        )
+        skp_sb = stage.tile([P, B, DIL], F32)
+        nc.scalar.copy(out=skp_sb[:].rearrange("p b t -> p (b t)"), in_=skp_sum[:])
+        nc.sync.dma_start(out=out_1.rearrange("b s t -> s b t"), in_=skp_sb[:])

@@ -36,12 +36,21 @@ def tile_gatedresidualcondconv_pa_s_kernel(
         mx = ctx.enter_context(tc.tile_pool(name="mx", bufs=1))
         turned = ctx.enter_context(tc.psum_pool(name="turned", bufs=6))
         sums = ctx.enter_context(tc.psum_pool(name="sums", bufs=2))
+        ctx.enter_context(tc.manual_schedule())
 
         ident = const.tile([P, P], F32)
         make_identity(nc, ident[:])
         warm = const.tile([P, 1], F32)
         nc.vector.memset(warm[:], 0.0)
         nc.scalar.activation(out=warm[:], in_=warm[:], func=ACT.Sigmoid)
+
+        bias_rows = const.tile([P, P], F32)
+        nc.vector.memset(bias_rows[:], 0.0)
+        for g, b_vec in enumerate((b_sig, b_gate)):
+            nc.sync.dma_start(
+                out=bias_rows[g * HALVES : (g + 1) * HALVES, :].bitcast(BF16),
+                in_=b_vec.rearrange("(u w) -> u w", u=HALVES),
+            )
 
         def load(name, shape, view):
             rows = raw.tile(shape, BF16, name=name)
@@ -56,36 +65,26 @@ def tile_gatedresidualcondconv_pa_s_kernel(
 
         sig_rows = [None] * PACK
         gate_rows = [None] * PACK
+        psig_rows = [None] * HALVES
+        pgate_rows = [None] * HALVES
         sig_rows[0] = load("sig0", [P, TAPS * CH], sig_view[:, 0, 0, :])
-        x_sb = load("x_sb", [P, B * PACK, T], x.rearrange("b (j p) t -> p (b j) t", p=P))
+        psig_rows[0] = load("psig0", [P, 2, CH], psig_view[:, 0])
         gate_rows[0] = load("gate0", [P, TAPS * CH], gate_view[:, 0, 0, :])
+        pgate_rows[0] = load("pgate0", [P, 2, CH], pgate_view[:, 0])
+        sig_rows[1] = load("sig1", [P, TAPS * CH], sig_view[:, 0, 1, :])
+        x_sb = load("x_sb", [P, B * PACK, T], x.rearrange("b (j p) t -> p (b j) t", p=P))
+        gate_rows[1] = load("gate1", [P, TAPS * CH], gate_view[:, 0, 1, :])
         c_sb = load(
             "c_sb", [P, B * HALVES, 2 * T], cond.rearrange("b (u p e) t -> p (b u) (e t)", u=HALVES, e=2)
         )
-        sig_rows[1] = load("sig1", [P, TAPS * CH], sig_view[:, 0, 1, :])
-        psig_rows = [load("psig0", [P, 2, CH], psig_view[:, 0])]
-        gate_rows[1] = load("gate1", [P, TAPS * CH], gate_view[:, 0, 1, :])
-        pgate_rows = [load("pgate0", [P, 2, CH], pgate_view[:, 0])]
         sig_rows[2] = load("sig2", [P, TAPS * CH], sig_view[:, 1, 0, :])
-        psig_rows.append(load("psig1", [P, 2, CH], psig_view[:, 1]))
+        psig_rows[1] = load("psig1", [P, 2, CH], psig_view[:, 1])
         gate_rows[2] = load("gate2", [P, TAPS * CH], gate_view[:, 1, 0, :])
-        pgate_rows.append(load("pgate1", [P, 2, CH], pgate_view[:, 1]))
+        pgate_rows[1] = load("pgate1", [P, 2, CH], pgate_view[:, 1])
         sig_rows[3] = load("sig3", [P, TAPS * CH], sig_view[:, 1, 1, :])
-        res_rows = [load("res0", [P, 2, CH], res_view[:, 0])]
         gate_rows[3] = load("gate3", [P, TAPS * CH], gate_view[:, 1, 1, :])
-        res_rows.append(load("res1", [P, 2, CH], res_view[:, 1]))
+        res_rows = [load("res%d" % h, [P, 2, CH], res_view[:, h]) for h in range(2)]
         skp_rows = load("skp", [P, 1, CH], w_skp.rearrange("s (o d) -> s o d", o=1))
-
-        bias_sig = const.tile([P, PACK], BF16)
-        nc.scalar.dma_start(
-            out=bias_sig[:].rearrange("p (u e) -> p u e", u=HALVES),
-            in_=b_sig.rearrange("(u p e) -> p u e", u=HALVES, e=2),
-        )
-        bias_gate = const.tile([P, PACK], BF16)
-        nc.scalar.dma_start(
-            out=bias_gate[:].rearrange("p (u e) -> p u e", u=HALVES),
-            in_=b_gate.rearrange("(u p e) -> p u e", u=HALVES, e=2),
-        )
 
         def quantise(name, grouped_flat, columns):
             codes = mx.tile([P, columns], U32, name=name + "_codes", align_bytes=64)
@@ -93,28 +92,24 @@ def tile_gatedresidualcondconv_pa_s_kernel(
             nc.vector.quantize_mx(out=codes[:].bitcast(FP8X4), scales=scales[:], in_=grouped_flat)
             return codes, scales
 
-        def tap_weights(name, rows):
+        def turn_taps(name, rows, empty_bank):
             words = rows[:].bitcast(F32)
             bank = turned.tile([P, PACK, P], F32, tag="bank", name=name + "_bank")
             for j in range(PACK):
                 nc.tensor.transpose(bank[:, j, :], words[:, j * P : (j + 1) * P], ident[:])
             grouped = stage.tile([P, TAPS, P, PACK], BF16, name=name + "_grouped", align_bytes=64)
-            nc.scalar.copy(
-                out=grouped[:], in_=bank[:].bitcast(BF16).rearrange("p j (m t) -> p t m j", t=TAPS)
-            )
-            return quantise(name, grouped[:].rearrange("p t m j -> p (t m j)"), TAPS * P)
+            empty_bank(out=grouped[:], in_=bank[:].bitcast(BF16).rearrange("p j (m t) -> p t m j", t=TAPS))
+            return grouped[:].rearrange("p t m j -> p (t m j)")
 
-        def plain_weights(name, rows, chunks):
+        def turn_plain(name, rows, chunks, empty_bank):
             bank = turned.tile([P, chunks, HALVES, P], F32, tag="bank", name=name + "_bank")
             for i in range(chunks):
                 words = rows[:, i, :].bitcast(F32)
                 for v in range(HALVES):
                     nc.tensor.transpose(bank[:, i, v, :], words[:, v * P : (v + 1) * P], ident[:])
             grouped = stage.tile([P, chunks, P, PACK], BF16, name=name + "_grouped", align_bytes=64)
-            nc.vector.tensor_copy(
-                out=grouped[:].bitcast(F32), in_=bank[:].rearrange("p i v m -> p i m v")
-            )
-            return quantise(name, grouped[:].rearrange("p i m t -> p (i m t)"), chunks * P)
+            empty_bank(out=grouped[:].bitcast(F32), in_=bank[:].rearrange("p i v m -> p i m v"))
+            return grouped[:].rearrange("p i m t -> p (i m t)")
 
         def mx_pass(out, weights, first, moving, moving_first, start, stop):
             w_codes, w_scales = weights
@@ -129,44 +124,84 @@ def tile_gatedresidualcondconv_pa_s_kernel(
                 stop=stop,
             )
 
+        tanh_filt = stage.tile([P, PACK, N], F32)
+        sigm_gate = stage.tile([P, PACK, N], F32)
+
+        def gated_chunk(s):
+            acc = sums.tile([P, 2, N], F32, tag="sum", name="acc%d" % s)
+            for g, (taps_mx, proj_mx) in enumerate(((sig_mx[s], psig_mx[s // 2]), (gate_mx[s], pgate_mx[s // 2]))):
+                mx_pass(acc[:, g, :], taps_mx, 0, x_mx, 0, True, False)
+                mx_pass(acc[:, g, :], taps_mx, P, x_mx, N, False, False)
+                mx_pass(acc[:, g, :], proj_mx, (s % 2) * P, c_mx, 0, False, True)
+            nc.scalar.activation(
+                out=tanh_filt[:, s, :], in_=acc[:, 0, :], func=ACT.Tanh, bias=bias[:, 0, s : s + 1]
+            )
+            nc.scalar.activation(
+                out=sigm_gate[:, s, :], in_=acc[:, 1, :], func=ACT.Sigmoid, bias=bias[:, 1, s : s + 1]
+            )
+
+        sig_mx = [None] * PACK
+        gate_mx = [None] * PACK
+        psig_mx = [None] * HALVES
+        pgate_mx = [None] * HALVES
+        by_scalar = nc.scalar.copy
+        by_vector = nc.vector.tensor_copy
+
+        bias_bank = turned.tile([P, P], F32, tag="bank")
+        nc.tensor.transpose(bias_bank[:], bias_rows[:], ident[:])
+        bias = const.tile([P, 2, PACK], BF16)
+        nc.vector.tensor_copy(
+            out=bias[:].rearrange("p g s -> p (g s)").bitcast(F32), in_=bias_bank[:, 0 : 2 * HALVES]
+        )
+
+        sig_g = turn_taps("sig0", sig_rows[0], by_scalar)
+        proj_g = turn_plain("psig0", psig_rows[0], 2, by_vector)
+        sig_mx[0] = quantise("sig0", sig_g, TAPS * P)
+        psig_mx[0] = quantise("psig0", proj_g, 2 * P)
+
+        gate_g = turn_taps("gate0", gate_rows[0], by_scalar)
+        proj_g = turn_plain("pgate0", pgate_rows[0], 2, by_vector)
+        gate_mx[0] = quantise("gate0", gate_g, TAPS * P)
+        pgate_mx[0] = quantise("pgate0", proj_g, 2 * P)
+
+        sig_g = turn_taps("sig1", sig_rows[1], by_scalar)
         x_grouped = stage.tile([P, TAPS, B, DIL, PACK], BF16, align_bytes=64)
         x_by_time = x_sb[:].rearrange("p (b j) t -> p b t j", b=B)
         for h in range(TAPS):
             nc.vector.tensor_copy(out=x_grouped[:, h], in_=x_by_time[:, :, h * DIL : (h + 1) * DIL, :])
         x_mx = quantise("x", x_grouped[:].rearrange("p h b t j -> p (h b t j)"), TAPS * N)
+        sig_mx[1] = quantise("sig1", sig_g, TAPS * P)
 
+        gate_g = turn_taps("gate1", gate_rows[1], by_scalar)
         c_grouped = stage.tile([P, B, DIL, PACK], BF16, align_bytes=64)
         c_by_time = c_sb[:].rearrange("p (b u) (e t) -> p b t (u e)", b=B, e=2)
         nc.vector.tensor_copy(out=c_grouped[:], in_=c_by_time[:, :, DIL:T, :])
         c_mx = quantise("c", c_grouped[:].rearrange("p b t s -> p (b t s)"), N)
+        gate_mx[1] = quantise("gate1", gate_g, TAPS * P)
 
-        tanh_filt = stage.tile([P, PACK, N], F32)
-        sigm_gate = stage.tile([P, PACK, N], F32)
-        for u in range(HALVES):
-            sig_mx = [None, None]
-            gate_mx = [None, None]
-            for e in range(2):
-                s = 2 * u + e
-                sig_mx[e] = tap_weights("sig%d" % s, sig_rows[s])
-                gate_mx[e] = tap_weights("gate%d" % s, gate_rows[s])
-            psig_mx = plain_weights("psig%d" % u, psig_rows[u], 2)
-            pgate_mx = plain_weights("pgate%d" % u, pgate_rows[u], 2)
-            for e in range(2):
-                s = 2 * u + e
-                acc = sums.tile([P, 2, N], F32, tag="sum", name="acc%d" % s)
-                for g, (taps_mx, proj_mx) in enumerate(((sig_mx[e], psig_mx), (gate_mx[e], pgate_mx))):
-                    mx_pass(acc[:, g, :], taps_mx, 0, x_mx, 0, True, False)
-                    mx_pass(acc[:, g, :], taps_mx, P, x_mx, N, False, False)
-                    mx_pass(acc[:, g, :], proj_mx, e * P, c_mx, 0, False, True)
-                nc.scalar.activation(
-                    out=sigm_gate[:, s, :], in_=acc[:, 1, :], func=ACT.Sigmoid, bias=bias_gate[:, s : s + 1]
-                )
-                nc.scalar.activation(
-                    out=tanh_filt[:, s, :], in_=acc[:, 0, :], func=ACT.Tanh, bias=bias_sig[:, s : s + 1]
-                )
+        sig_g = turn_taps("sig2", sig_rows[2], by_scalar)
+        proj_g = turn_plain("psig1", psig_rows[1], 2, by_vector)
+        sig_mx[2] = quantise("sig2", sig_g, TAPS * P)
+        psig_mx[1] = quantise("psig1", proj_g, 2 * P)
 
-        res_mx = [plain_weights("res%d" % h, res_rows[h], 2) for h in range(2)]
-        skp_mx = plain_weights("skp", skp_rows, 1)
+        gate_g = turn_taps("gate2", gate_rows[2], by_scalar)
+        proj_g = turn_plain("pgate1", pgate_rows[1], 2, by_vector)
+        gate_mx[2] = quantise("gate2", gate_g, TAPS * P)
+        pgate_mx[1] = quantise("pgate1", proj_g, 2 * P)
+        gated_chunk(0)
+        gated_chunk(1)
+
+        sig_g = turn_taps("sig3", sig_rows[3], by_vector)
+        gate_g = turn_taps("gate3", gate_rows[3], by_scalar)
+        sig_mx[3] = quantise("sig3", sig_g, TAPS * P)
+        gate_mx[3] = quantise("gate3", gate_g, TAPS * P)
+        gated_chunk(2)
+
+        res_g = [turn_plain("res%d" % h, res_rows[h], 2, by_scalar) for h in range(2)]
+        skp_g = turn_plain("skp", skp_rows, 1, by_vector)
+        res_mx = [quantise("res%d" % h, res_g[h], 2 * P) for h in range(2)]
+        skp_mx = quantise("skp", skp_g, P)
+        gated_chunk(3)
 
         z_grouped = stage.tile([P, N, PACK], BF16, align_bytes=64)
         nc.vector.tensor_tensor(
@@ -177,23 +212,18 @@ def tile_gatedresidualcondconv_pa_s_kernel(
         )
         z_mx = quantise("z", z_grouped[:].rearrange("p n s -> p (n s)"), N)
 
-        res_sum = sums.tile([P, PACK, N], F32, tag="sum")
+        res_sum = sums.tile([P, PACK, B, DIL], F32, tag="sum")
         for j in range(PACK):
-            mx_pass(res_sum[:, j, :], res_mx[j // 2], (j % 2) * P, z_mx, 0, True, True)
+            mx_pass(res_sum[:, j].rearrange("p b t -> p (b t)"), res_mx[j // 2], (j % 2) * P, z_mx, 0, True, True)
         skp_sum = sums.tile([P, N], F32, tag="sum")
         mx_pass(skp_sum[:], skp_mx, 0, z_mx, 0, True, True)
 
-        sig_sb = stage.tile([P, B, PACK, DIL], F32)
-        nc.vector.tensor_tensor(
-            out=sig_sb[:].rearrange("p b j t -> p j b t"),
-            in0=res_sum[:].rearrange("p j (b t) -> p j b t", b=B),
-            in1=x_sb[:].rearrange("p (b j) t -> p j b t", b=B)[:, :, :, DIL:T],
-            op=ALU.add,
-        )
-        nc.sync.dma_start(
-            out=out_0.rearrange("b (j p) t -> p (b j) t", p=P),
-            in_=sig_sb[:].rearrange("p b j t -> p (b j) t"),
-        )
         skp_sb = stage.tile([P, B, DIL], F32)
         nc.scalar.copy(out=skp_sb[:].rearrange("p b t -> p (b t)"), in_=skp_sum[:])
         nc.sync.dma_start(out=out_1.rearrange("b s t -> s b t"), in_=skp_sb[:])
+
+        x_later = x_sb[:].rearrange("p (b j) t -> p b j t", b=B)[:, :, :, DIL:T]
+        sig_sb = stage.tile([P, B, PACK, DIL], F32)
+        for b in range(B):
+            nc.vector.tensor_tensor(out=sig_sb[:, b], in0=res_sum[:, :, b, :], in1=x_later[:, b], op=ALU.add)
+            nc.sync.dma_start(out=out_0[b].rearrange("(j p) t -> p j t", p=P), in_=sig_sb[:, b])

@@ -46,11 +46,6 @@ def tile_gatedresidualcondconv_pa_s_kernel(
 
         bias_rows = const.tile([P, P], F32)
         nc.vector.memset(bias_rows[:], 0.0)
-        for g, b_vec in enumerate((b_sig, b_gate)):
-            nc.sync.dma_start(
-                out=bias_rows[g * HALVES : (g + 1) * HALVES, :].bitcast(BF16),
-                in_=b_vec.rearrange("(u w) -> u w", u=HALVES),
-            )
 
         def load(name, shape, view):
             rows = raw.tile(shape, BF16, name=name)
@@ -71,6 +66,11 @@ def tile_gatedresidualcondconv_pa_s_kernel(
         psig_rows[0] = load("psig0", [P, 2, CH], psig_view[:, 0])
         gate_rows[0] = load("gate0", [P, TAPS * CH], gate_view[:, 0, 0, :])
         pgate_rows[0] = load("pgate0", [P, 2, CH], pgate_view[:, 0])
+        for g, b_vec in enumerate((b_sig, b_gate)):
+            nc.sync.dma_start(
+                out=bias_rows[g * HALVES : (g + 1) * HALVES, :].bitcast(BF16),
+                in_=b_vec.rearrange("(u w) -> u w", u=HALVES),
+            )
         sig_rows[1] = load("sig1", [P, TAPS * CH], sig_view[:, 0, 1, :])
         x_sb = load("x_sb", [P, B * PACK, T], x.rearrange("b (j p) t -> p (b j) t", p=P))
         gate_rows[1] = load("gate1", [P, TAPS * CH], gate_view[:, 0, 1, :])
@@ -147,13 +147,6 @@ def tile_gatedresidualcondconv_pa_s_kernel(
         by_scalar = nc.scalar.copy
         by_vector = nc.vector.tensor_copy
 
-        bias_bank = turned.tile([P, P], F32, tag="bank")
-        nc.tensor.transpose(bias_bank[:], bias_rows[:], ident[:])
-        bias = const.tile([P, 2, PACK], BF16)
-        nc.vector.tensor_copy(
-            out=bias[:].rearrange("p g s -> p (g s)").bitcast(F32), in_=bias_bank[:, 0 : 2 * HALVES]
-        )
-
         sig_g = turn_taps("sig0", sig_rows[0], by_scalar)
         proj_g = turn_plain("psig0", psig_rows[0], 2, by_vector)
         sig_mx[0] = quantise("sig0", sig_g, TAPS * P)
@@ -163,6 +156,13 @@ def tile_gatedresidualcondconv_pa_s_kernel(
         proj_g = turn_plain("pgate0", pgate_rows[0], 2, by_vector)
         gate_mx[0] = quantise("gate0", gate_g, TAPS * P)
         pgate_mx[0] = quantise("pgate0", proj_g, 2 * P)
+
+        bias_bank = turned.tile([P, P], F32, tag="bank")
+        nc.tensor.transpose(bias_bank[:], bias_rows[:], ident[:])
+        bias = const.tile([P, 2, PACK], BF16)
+        nc.vector.tensor_copy(
+            out=bias[:].rearrange("p g s -> p (g s)").bitcast(F32), in_=bias_bank[:, 0 : 2 * HALVES]
+        )
 
         sig_g = turn_taps("sig1", sig_rows[1], by_scalar)
         x_grouped = stage.tile([P, TAPS, B, DIL, PACK], BF16, align_bytes=64)

@@ -20,6 +20,7 @@ T = 128
 DIL = 64
 TAPS = 2
 N = B * DIL
+GROUPS = 4
 HALVES = 2
 
 FLOPS = 2 * N * (6 * CH * CH + CH * CH + SKIP * CH)
@@ -40,6 +41,8 @@ def tile_gatedresidualcondconv_pa_s_kernel(
 
         ident = const.tile([P, P], F32)
         make_identity(nc, ident[:])
+        ident_bf = const.tile([P, P], BF16)
+        nc.vector.tensor_copy(out=ident_bf[:], in_=ident[:])
         warm = const.tile([P, 1], F32)
         nc.vector.memset(warm[:], 0.0)
         nc.scalar.activation(out=warm[:], in_=warm[:], func=ACT.Sigmoid)
@@ -52,39 +55,39 @@ def tile_gatedresidualcondconv_pa_s_kernel(
             nc.sync.dma_start(out=rows[:], in_=view)
             return rows
 
-        sig_view = w_sig.rearrange("(u p e) r t -> p u e (r t)", u=HALVES, e=2)
-        gate_view = w_gate.rearrange("(u p e) r t -> p u e (r t)", u=HALVES, e=2)
+        sig_view = w_sig.rearrange("(u g d) (h r) t -> u (d h) g (r t)", u=HALVES, g=GROUPS, h=2)
+        gate_view = w_gate.rearrange("(u g d) (h r) t -> u (d h) g (r t)", u=HALVES, g=GROUPS, h=2)
         psig_view = w_psig.rearrange("(u p e) c -> p u e c", u=HALVES, e=2)
         pgate_view = w_pgate.rearrange("(u p e) c -> p u e c", u=HALVES, e=2)
-        res_view = w_res.rearrange("(h i p) d -> p h i d", h=2, i=2)
+        res_view = w_res.rearrange("(p h i) d -> p h i d", h=2, i=2)
 
-        sig_rows = [None] * PACK
-        gate_rows = [None] * PACK
+        def load_taps(name, view):
+            return [load("%s_%d" % (name, b), [P, 2, CH], view[:, 2 * b : 2 * b + 2, :]) for b in range(2)]
+
+        sig_rows = [None] * HALVES
+        gate_rows = [None] * HALVES
         psig_rows = [None] * HALVES
         pgate_rows = [None] * HALVES
-        sig_rows[0] = load("sig0", [P, TAPS * CH], sig_view[:, 0, 0, :])
         psig_rows[0] = load("psig0", [P, 2, CH], psig_view[:, 0])
-        gate_rows[0] = load("gate0", [P, TAPS * CH], gate_view[:, 0, 0, :])
+        sig_rows[0] = load_taps("sig0", sig_view[0])
+        x_sb = load("x_sb", [P, B * 2, 2 * T], x.rearrange("b (h p v) t -> p (b h) (v t)", h=2, p=P))
         pgate_rows[0] = load("pgate0", [P, 2, CH], pgate_view[:, 0])
         for g, b_vec in enumerate((b_sig, b_gate)):
             nc.sync.dma_start(
                 out=bias_rows[g * HALVES : (g + 1) * HALVES, :].bitcast(BF16),
                 in_=b_vec.rearrange("(u w) -> u w", u=HALVES),
             )
-        sig_rows[1] = load("sig1", [P, TAPS * CH], sig_view[:, 0, 1, :])
-        x_sb = load("x_sb", [P, B * PACK, T], x.rearrange("b (j p) t -> p (b j) t", p=P))
-        gate_rows[1] = load("gate1", [P, TAPS * CH], gate_view[:, 0, 1, :])
+        gate_rows[0] = load_taps("gate0", gate_view[0])
         c_sb = load(
             "c_sb", [P, B * HALVES, 2 * T], cond.rearrange("b (u p e) t -> p (b u) (e t)", u=HALVES, e=2)
         )
-        sig_rows[2] = load("sig2", [P, TAPS * CH], sig_view[:, 1, 0, :])
         psig_rows[1] = load("psig1", [P, 2, CH], psig_view[:, 1])
-        gate_rows[2] = load("gate2", [P, TAPS * CH], gate_view[:, 1, 0, :])
+        sig_rows[1] = load_taps("sig1", sig_view[1])
         pgate_rows[1] = load("pgate1", [P, 2, CH], pgate_view[:, 1])
-        sig_rows[3] = load("sig3", [P, TAPS * CH], sig_view[:, 1, 1, :])
-        gate_rows[3] = load("gate3", [P, TAPS * CH], gate_view[:, 1, 1, :])
+        gate_rows[1] = load_taps("gate1", gate_view[1])
         res_rows = [load("res%d" % h, [P, 2, CH], res_view[:, h]) for h in range(2)]
         skp_rows = load("skp", [P, 1, CH], w_skp.rearrange("s (o d) -> s o d", o=1))
+        x_res = load("x_res", [P, B, PACK * T], x.rearrange("b (p j) t -> p b (j t)", j=PACK))
 
         def quantise(name, grouped_flat, columns):
             codes = mx.tile([P, columns], U32, name=name + "_codes", align_bytes=64)
@@ -92,14 +95,19 @@ def tile_gatedresidualcondconv_pa_s_kernel(
             nc.vector.quantize_mx(out=codes[:].bitcast(FP8X4), scales=scales[:], in_=grouped_flat)
             return codes, scales
 
-        def turn_taps(name, rows, empty_bank):
-            words = rows[:].bitcast(F32)
-            bank = turned.tile([P, PACK, P], F32, tag="bank", name=name + "_bank")
-            for j in range(PACK):
-                nc.tensor.transpose(bank[:, j, :], words[:, j * P : (j + 1) * P], ident[:])
-            grouped = stage.tile([P, TAPS, P, PACK], BF16, name=name + "_grouped", align_bytes=64)
-            empty_bank(out=grouped[:], in_=bank[:].bitcast(BF16).rearrange("p j (m t) -> p t m j", t=TAPS))
-            return grouped[:].rearrange("p t m j -> p (t m j)")
+        def turn_tap(name, rows, tap, empty_bank):
+            bank = turned.tile([P, 2, GROUPS, P], BF16, tag="bank", name=name + "_bank")
+            for g in range(GROUPS):
+                for v in range(2):
+                    nc.tensor.transpose(
+                        bank[:, v, g, :],
+                        rows[g // 2][:, g % 2, 2 * v + tap :: 2 * TAPS],
+                        ident_bf[:],
+                    )
+            grouped = stage.tile([P, 2, P, PACK], BF16, name=name + "_grouped", align_bytes=64)
+            words = bank[:].rearrange("p v g i -> p (v g i)").bitcast(F32)
+            empty_bank(out=grouped[:].bitcast(F32), in_=words.rearrange("p (v m e) -> p e m v", v=2, e=2))
+            return grouped[:].rearrange("p e m s -> p (e m s)")
 
         def turn_plain(name, rows, chunks, empty_bank):
             bank = turned.tile([P, chunks, HALVES, P], F32, tag="bank", name=name + "_bank")
@@ -127,81 +135,70 @@ def tile_gatedresidualcondconv_pa_s_kernel(
         tanh_filt = stage.tile([P, PACK, N], F32)
         sigm_gate = stage.tile([P, PACK, N], F32)
 
-        def gated_chunk(s):
-            acc = sums.tile([P, 2, N], F32, tag="sum", name="acc%d" % s)
-            for g, (taps_mx, proj_mx) in enumerate(((sig_mx[s], psig_mx[s // 2]), (gate_mx[s], pgate_mx[s // 2]))):
-                mx_pass(acc[:, g, :], taps_mx, 0, x_mx, 0, True, False)
-                mx_pass(acc[:, g, :], taps_mx, P, x_mx, N, False, False)
-                mx_pass(acc[:, g, :], proj_mx, (s % 2) * P, c_mx, 0, False, True)
-            nc.scalar.activation(
-                out=tanh_filt[:, s, :], in_=acc[:, 0, :], func=ACT.Tanh, bias=bias[:, 0, s : s + 1]
-            )
-            nc.scalar.activation(
-                out=sigm_gate[:, s, :], in_=acc[:, 1, :], func=ACT.Sigmoid, bias=bias[:, 1, s : s + 1]
-            )
+        def branch(g, u, taps_mx, proj_mx):
+            acc = sums.tile([P, 2, N], F32, tag="sum", name="acc%d%d" % (g, u))
+            for e in range(2):
+                mx_pass(acc[:, e, :], proj_mx, e * P, c_mx, 0, True, False)
+                mx_pass(acc[:, e, :], taps_mx[0], e * P, x_mx, 0, False, False)
+                mx_pass(acc[:, e, :], taps_mx[1], e * P, x_mx, N, False, True)
+            for e in range(2):
+                s = 2 * u + e
+                nc.scalar.activation(
+                    out=(tanh_filt, sigm_gate)[g][:, s, :],
+                    in_=acc[:, e, :],
+                    func=(ACT.Tanh, ACT.Sigmoid)[g],
+                    bias=bias[:, g, s : s + 1],
+                )
 
-        sig_mx = [None] * PACK
-        gate_mx = [None] * PACK
-        psig_mx = [None] * HALVES
-        pgate_mx = [None] * HALVES
         by_scalar = nc.scalar.copy
         by_vector = nc.vector.tensor_copy
 
-        sig_g = turn_taps("sig0", sig_rows[0], by_scalar)
-        proj_g = turn_plain("psig0", psig_rows[0], 2, by_vector)
-        sig_mx[0] = quantise("sig0", sig_g, TAPS * P)
-        psig_mx[0] = quantise("psig0", proj_g, 2 * P)
+        psig_g = turn_plain("psig0", psig_rows[0], 2, by_scalar)
+        sig_g = [turn_tap("sig0%d" % t, sig_rows[0], t, by_scalar) for t in range(TAPS)]
+        psig0_mx = quantise("psig0", psig_g, 2 * P)
+        x_grouped = stage.tile([P, TAPS, B, DIL, 2, 2], BF16, align_bytes=64)
+        x_by_time = x_sb[:].rearrange("p (b h) (v t) -> p b t v h", b=B, v=2)
+        for tap in range(TAPS):
+            nc.vector.tensor_copy(out=x_grouped[:, tap], in_=x_by_time[:, :, tap * DIL : (tap + 1) * DIL])
+        sig0_mx = [quantise("sig00", sig_g[0], 2 * P)]
+        x_mx = quantise("x", x_grouped[:].rearrange("p h b t v j -> p (h b t v j)"), TAPS * N)
+        sig0_mx.append(quantise("sig01", sig_g[1], 2 * P))
 
-        gate_g = turn_taps("gate0", gate_rows[0], by_scalar)
-        proj_g = turn_plain("pgate0", pgate_rows[0], 2, by_vector)
-        gate_mx[0] = quantise("gate0", gate_g, TAPS * P)
-        pgate_mx[0] = quantise("pgate0", proj_g, 2 * P)
-
+        pgate_g = turn_plain("pgate0", pgate_rows[0], 2, by_vector)
         bias_bank = turned.tile([P, P], F32, tag="bank")
         nc.tensor.transpose(bias_bank[:], bias_rows[:], ident[:])
+        gate_g = [turn_tap("gate0%d" % t, gate_rows[0], t, by_scalar) for t in range(TAPS)]
         bias = const.tile([P, 2, PACK], BF16)
         nc.vector.tensor_copy(
             out=bias[:].rearrange("p g s -> p (g s)").bitcast(F32), in_=bias_bank[:, 0 : 2 * HALVES]
         )
-
-        sig_g = turn_taps("sig1", sig_rows[1], by_scalar)
-        x_grouped = stage.tile([P, TAPS, B, DIL, PACK], BF16, align_bytes=64)
-        x_by_time = x_sb[:].rearrange("p (b j) t -> p b t j", b=B)
-        for h in range(TAPS):
-            nc.vector.tensor_copy(out=x_grouped[:, h], in_=x_by_time[:, :, h * DIL : (h + 1) * DIL, :])
-        x_mx = quantise("x", x_grouped[:].rearrange("p h b t j -> p (h b t j)"), TAPS * N)
-        sig_mx[1] = quantise("sig1", sig_g, TAPS * P)
-
-        gate_g = turn_taps("gate1", gate_rows[1], by_scalar)
         c_grouped = stage.tile([P, B, DIL, PACK], BF16, align_bytes=64)
         c_by_time = c_sb[:].rearrange("p (b u) (e t) -> p b t (u e)", b=B, e=2)
         nc.vector.tensor_copy(out=c_grouped[:], in_=c_by_time[:, :, DIL:T, :])
+        pgate0_mx = quantise("pgate0", pgate_g, 2 * P)
+        gate0_mx = [quantise("gate00", gate_g[0], 2 * P)]
         c_mx = quantise("c", c_grouped[:].rearrange("p b t s -> p (b t s)"), N)
-        gate_mx[1] = quantise("gate1", gate_g, TAPS * P)
+        gate0_mx.append(quantise("gate01", gate_g[1], 2 * P))
 
-        sig_g = turn_taps("sig2", sig_rows[2], by_scalar)
-        proj_g = turn_plain("psig1", psig_rows[1], 2, by_vector)
-        sig_mx[2] = quantise("sig2", sig_g, TAPS * P)
-        psig_mx[1] = quantise("psig1", proj_g, 2 * P)
+        psig_g = turn_plain("psig1", psig_rows[1], 2, by_scalar)
+        sig_g = [turn_tap("sig1%d" % t, sig_rows[1], t, by_scalar) for t in range(TAPS)]
+        branch(0, 0, sig0_mx, psig0_mx)
+        psig1_mx = quantise("psig1", psig_g, 2 * P)
+        sig1_mx = [quantise("sig10", sig_g[0], 2 * P)]
 
-        gate_g = turn_taps("gate2", gate_rows[2], by_scalar)
-        proj_g = turn_plain("pgate1", pgate_rows[1], 2, by_vector)
-        gate_mx[2] = quantise("gate2", gate_g, TAPS * P)
-        pgate_mx[1] = quantise("pgate1", proj_g, 2 * P)
-        gated_chunk(0)
-        gated_chunk(1)
+        pgate_g = turn_plain("pgate1", pgate_rows[1], 2, by_vector)
+        sig1_mx.append(quantise("sig11", sig_g[1], 2 * P))
+        gate_g = [turn_tap("gate1%d" % t, gate_rows[1], t, by_scalar) for t in range(TAPS)]
+        branch(1, 0, gate0_mx, pgate0_mx)
+        pgate1_mx = quantise("pgate1", pgate_g, 2 * P)
+        gate1_mx = [quantise("gate1%d" % t, gate_g[t], 2 * P) for t in range(TAPS)]
+        branch(0, 1, sig1_mx, psig1_mx)
 
-        sig_g = turn_taps("sig3", sig_rows[3], by_vector)
-        gate_g = turn_taps("gate3", gate_rows[3], by_scalar)
-        sig_mx[3] = quantise("sig3", sig_g, TAPS * P)
-        gate_mx[3] = quantise("gate3", gate_g, TAPS * P)
-        gated_chunk(2)
-
-        res_g = [turn_plain("res%d" % h, res_rows[h], 2, by_scalar) for h in range(2)]
-        skp_g = turn_plain("skp", skp_rows, 1, by_vector)
+        res_g = [turn_plain("res%d" % h, res_rows[h], 2, (by_scalar, by_vector)[h]) for h in range(2)]
+        branch(1, 1, gate1_mx, pgate1_mx)
+        skp_g = turn_plain("skp", skp_rows, 1, by_scalar)
         res_mx = [quantise("res%d" % h, res_g[h], 2 * P) for h in range(2)]
         skp_mx = quantise("skp", skp_g, P)
-        gated_chunk(3)
 
         z_grouped = stage.tile([P, N, PACK], BF16, align_bytes=64)
         nc.vector.tensor_tensor(
@@ -222,8 +219,8 @@ def tile_gatedresidualcondconv_pa_s_kernel(
         nc.scalar.copy(out=skp_sb[:].rearrange("p b t -> p (b t)"), in_=skp_sum[:])
         nc.sync.dma_start(out=out_1.rearrange("b s t -> s b t"), in_=skp_sb[:])
 
-        x_later = x_sb[:].rearrange("p (b j) t -> p b j t", b=B)[:, :, :, DIL:T]
+        x_later = x_res[:].rearrange("p b (j t) -> p b j t", j=PACK)[:, :, :, DIL:T]
         sig_sb = stage.tile([P, B, PACK, DIL], F32)
         for b in range(B):
             nc.vector.tensor_tensor(out=sig_sb[:, b], in0=res_sum[:, :, b, :], in1=x_later[:, b], op=ALU.add)
-            nc.sync.dma_start(out=out_0[b].rearrange("(j p) t -> p j t", p=P), in_=sig_sb[:, b])
+            nc.sync.dma_start(out=out_0[b].rearrange("(p j) t -> p (j t)", j=PACK), in_=sig_sb[:, b].rearrange("p j t -> p (j t)"))

@@ -70,7 +70,7 @@ def tile_gatedresidualcondconv_pa_s_kernel(
         pgate_rows = [None] * HALVES
         psig_rows[0] = load("psig0", [P, 2, CH], psig_view[:, 0])
         sig_rows[0] = load_taps("sig0", sig_view[0])
-        x_sb = load("x_sb", [P, B * 2, 2 * T], x.rearrange("b (h p v) t -> p (b h) (v t)", h=2, p=P))
+        x_sb = load("x_sb", [P, B * PACK, T], x.rearrange("b (h v p) t -> p (b h v) t", h=2, p=P))
         pgate_rows[0] = load("pgate0", [P, 2, CH], pgate_view[:, 0])
         for g, b_vec in enumerate((b_sig, b_gate)):
             nc.sync.dma_start(
@@ -101,7 +101,7 @@ def tile_gatedresidualcondconv_pa_s_kernel(
                 for v in range(2):
                     nc.tensor.transpose(
                         bank[:, v, g, :],
-                        rows[g // 2][:, g % 2, 2 * v + tap :: 2 * TAPS],
+                        rows[g // 2][:, g % 2, 2 * P * v + tap : 2 * P * (v + 1) : TAPS],
                         ident_bf[:],
                     )
             grouped = stage.tile([P, 2, P, PACK], BF16, name=name + "_grouped", align_bytes=64)
@@ -157,7 +157,7 @@ def tile_gatedresidualcondconv_pa_s_kernel(
         sig_g = [turn_tap("sig0%d" % t, sig_rows[0], t, by_scalar) for t in range(TAPS)]
         psig0_mx = quantise("psig0", psig_g, 2 * P)
         x_grouped = stage.tile([P, TAPS, B, DIL, 2, 2], BF16, align_bytes=64)
-        x_by_time = x_sb[:].rearrange("p (b h) (v t) -> p b t v h", b=B, v=2)
+        x_by_time = x_sb[:].rearrange("p (b h v) t -> p b t v h", b=B, h=2)
         for tap in range(TAPS):
             nc.vector.tensor_copy(out=x_grouped[:, tap], in_=x_by_time[:, :, tap * DIL : (tap + 1) * DIL])
         sig0_mx = [quantise("sig00", sig_g[0], 2 * P)]

@@ -35,20 +35,31 @@ def tile_gatedresidualcondconv_pa_s_kernel(
         raw = ctx.enter_context(tc.tile_pool(name="raw", bufs=1))
         stage = ctx.enter_context(tc.tile_pool(name="stage", bufs=1))
         mx = ctx.enter_context(tc.tile_pool(name="mx", bufs=1))
-        turned = ctx.enter_context(tc.psum_pool(name="turned", bufs=6))
+        turned = ctx.enter_context(tc.psum_pool(name="turned", bufs=5))
+        spare_pool = ctx.enter_context(tc.psum_pool(name="spare", bufs=1))
         sums = ctx.enter_context(tc.psum_pool(name="sums", bufs=2))
         ctx.enter_context(tc.manual_schedule())
 
+        zeros = const.tile([P, P], F32)
+        nc.vector.memset(zeros[:], 0.0)
+        spare = spare_pool.tile([P, P], F32)
+
+        def keep_clock(times):
+            for i in range(times):
+                nc.tensor.matmul(spare[:], lhsT=zeros[:], rhs=zeros[:], start=True, stop=True)
+
+        keep_clock(4)
+
         ident = const.tile([P, P], F32)
         make_identity(nc, ident[:])
-        ident_bf = const.tile([P, P], BF16)
-        nc.vector.tensor_copy(out=ident_bf[:], in_=ident[:])
         warm = const.tile([P, 1], F32)
         nc.vector.memset(warm[:], 0.0)
         nc.scalar.activation(out=warm[:], in_=warm[:], func=ACT.Sigmoid)
 
         bias_rows = const.tile([P, P], F32)
         nc.vector.memset(bias_rows[:], 0.0)
+        ident_bf = const.tile([P, P], BF16)
+        nc.vector.tensor_copy(out=ident_bf[:], in_=ident[:])
 
         def load(name, shape, view):
             rows = raw.tile(shape, BF16, name=name)
@@ -104,6 +115,8 @@ def tile_gatedresidualcondconv_pa_s_kernel(
                         rows[g // 2][:, g % 2, 2 * P * v + tap : 2 * P * (v + 1) : TAPS],
                         ident_bf[:],
                     )
+            if name != "gate11":
+                keep_clock(1)
             grouped = stage.tile([P, 2, P, PACK], BF16, name=name + "_grouped", align_bytes=64)
             words = bank[:].rearrange("p v g i -> p (v g i)").bitcast(F32)
             empty_bank(out=grouped[:].bitcast(F32), in_=words.rearrange("p (v m e) -> p e m v", v=2, e=2))

@@ -35,9 +35,9 @@ def tile_gatedresidualcondconv_pa_s_kernel(
         raw = ctx.enter_context(tc.tile_pool(name="raw", bufs=1))
         stage = ctx.enter_context(tc.tile_pool(name="stage", bufs=1))
         mx = ctx.enter_context(tc.tile_pool(name="mx", bufs=1))
-        turned = ctx.enter_context(tc.psum_pool(name="turned", bufs=5))
+        turned = ctx.enter_context(tc.psum_pool(name="turned", bufs=4))
         spare_pool = ctx.enter_context(tc.psum_pool(name="spare", bufs=1))
-        sums = ctx.enter_context(tc.psum_pool(name="sums", bufs=2))
+        sums = ctx.enter_context(tc.psum_pool(name="sums", bufs=3))
         ctx.enter_context(tc.manual_schedule())
 
         zeros = const.tile([P, P], F32)
@@ -48,7 +48,7 @@ def tile_gatedresidualcondconv_pa_s_kernel(
             for i in range(times):
                 nc.tensor.matmul(spare[:], lhsT=zeros[:], rhs=zeros[:], start=True, stop=True)
 
-        keep_clock(4)
+        keep_clock(3)
 
         ident = const.tile([P, P], F32)
         make_identity(nc, ident[:])
@@ -92,10 +92,10 @@ def tile_gatedresidualcondconv_pa_s_kernel(
         c_sb = load(
             "c_sb", [P, B * HALVES, 2 * T], cond.rearrange("b (u p e) t -> p (b u) (e t)", u=HALVES, e=2)
         )
-        psig_rows[1] = load("psig1", [P, 2, CH], psig_view[:, 1])
         sig_rows[1] = load_taps("sig1", sig_view[1])
-        pgate_rows[1] = load("pgate1", [P, 2, CH], pgate_view[:, 1])
+        psig_rows[1] = load("psig1", [P, 2, CH], psig_view[:, 1])
         gate_rows[1] = load_taps("gate1", gate_view[1])
+        pgate_rows[1] = load("pgate1", [P, 2, CH], pgate_view[:, 1])
         res_rows = [load("res%d" % h, [P, 2, CH], res_view[:, h]) for h in range(2)]
         skp_rows = load("skp", [P, 1, CH], w_skp.rearrange("s (o d) -> s o d", o=1))
         x_res = load("x_res", [P, B, PACK * T], x.rearrange("b (p j) t -> p b (j t)", j=PACK))
@@ -106,21 +106,24 @@ def tile_gatedresidualcondconv_pa_s_kernel(
             nc.vector.quantize_mx(out=codes[:].bitcast(FP8X4), scales=scales[:], in_=grouped_flat)
             return codes, scales
 
-        def turn_tap(name, rows, tap, empty_bank):
-            bank = turned.tile([P, 2, GROUPS, P], BF16, tag="bank", name=name + "_bank")
-            for g in range(GROUPS):
-                for v in range(2):
-                    nc.tensor.transpose(
-                        bank[:, v, g, :],
-                        rows[g // 2][:, g % 2, 2 * P * v + tap : 2 * P * (v + 1) : TAPS],
-                        ident_bf[:],
-                    )
-            if name != "gate11":
-                keep_clock(1)
-            grouped = stage.tile([P, 2, P, PACK], BF16, name=name + "_grouped", align_bytes=64)
-            words = bank[:].rearrange("p v g i -> p (v g i)").bitcast(F32)
-            empty_bank(out=grouped[:].bitcast(F32), in_=words.rearrange("p (v m e) -> p e m v", v=2, e=2))
-            return grouped[:].rearrange("p e m s -> p (e m s)")
+        def turn_taps(name, rows, empty_banks):
+            banks = [turned.tile([P, 2, GROUPS, P], BF16, tag="bank", name="%s%d_bank" % (name, t)) for t in range(TAPS)]
+            for half in range(2):
+                for tap in range(TAPS):
+                    for g in range(2):
+                        for v in range(2):
+                            nc.tensor.transpose(
+                                banks[tap][:, v, 2 * half + g, :],
+                                rows[half][:, g, 2 * P * v + tap : 2 * P * (v + 1) : TAPS],
+                                ident_bf[:],
+                            )
+            flat = []
+            for tap in range(TAPS):
+                grouped = stage.tile([P, 2, P, PACK], BF16, name="%s%d_grouped" % (name, tap), align_bytes=64)
+                words = banks[tap][:].rearrange("p v g i -> p (v g i)").bitcast(F32)
+                empty_banks[tap](out=grouped[:].bitcast(F32), in_=words.rearrange("p (v m e) -> p e m v", v=2, e=2))
+                flat.append(grouped[:].rearrange("p e m s -> p (e m s)"))
+            return flat
 
         def turn_plain(name, rows, chunks, empty_bank):
             bank = turned.tile([P, chunks, HALVES, P], F32, tag="bank", name=name + "_bank")
@@ -132,15 +135,15 @@ def tile_gatedresidualcondconv_pa_s_kernel(
             empty_bank(out=grouped[:].bitcast(F32), in_=bank[:].rearrange("p i v m -> p i m v"))
             return grouped[:].rearrange("p i m t -> p (i m t)")
 
-        def mx_pass(out, weights, first, moving, moving_first, start, stop):
+        def mx_pass(out, weights, first, moving, moving_first, start, stop, columns=N):
             w_codes, w_scales = weights
             m_codes, m_scales = moving
             nc.tensor.matmul_mx(
                 out=out,
                 lhsT=w_codes[:, first : first + P].bitcast(FP8X4),
                 lhsT_scale=w_scales[:, first : first + P],
-                rhs=m_codes[:, moving_first : moving_first + N].bitcast(FP8X4),
-                rhs_scale=m_scales[:, moving_first : moving_first + N],
+                rhs=m_codes[:, moving_first : moving_first + columns].bitcast(FP8X4),
+                rhs_scale=m_scales[:, moving_first : moving_first + columns],
                 start=start,
                 stop=stop,
             )
@@ -148,27 +151,32 @@ def tile_gatedresidualcondconv_pa_s_kernel(
         tanh_filt = stage.tile([P, PACK, N], F32)
         sigm_gate = stage.tile([P, PACK, N], F32)
 
-        def branch(g, u, taps_mx, proj_mx):
-            acc = sums.tile([P, 2, N], F32, tag="sum", name="acc%d%d" % (g, u))
-            for e in range(2):
-                mx_pass(acc[:, e, :], proj_mx, e * P, c_mx, 0, True, False)
-                mx_pass(acc[:, e, :], taps_mx[0], e * P, x_mx, 0, False, False)
-                mx_pass(acc[:, e, :], taps_mx[1], e * P, x_mx, N, False, True)
+        def gate_acts(g, u, accs):
             for e in range(2):
                 s = 2 * u + e
                 nc.scalar.activation(
                     out=(tanh_filt, sigm_gate)[g][:, s, :],
-                    in_=acc[:, e, :],
+                    in_=accs[e],
                     func=(ACT.Tanh, ACT.Sigmoid)[g],
                     bias=bias[:, g, s : s + 1],
                 )
+
+        def branch(g, u, taps_mx, proj_mx):
+            acc = sums.tile([P, 2, N], F32, tag="sum", name="acc%d%d" % (g, u))
+            for e in range(2):
+                mx_pass(acc[:, e, :], taps_mx[0], e * P, x_mx, 0, True, False)
+                mx_pass(acc[:, e, :], taps_mx[1], e * P, x_mx, N, False, False)
+                mx_pass(acc[:, e, :], proj_mx, e * P, c_mx, 0, False, True)
+            gate_acts(g, u, [acc[:, e, :] for e in range(2)])
 
         by_scalar = nc.scalar.copy
         by_vector = nc.vector.tensor_copy
 
         psig_g = turn_plain("psig0", psig_rows[0], 2, by_scalar)
-        sig_g = [turn_tap("sig0%d" % t, sig_rows[0], t, by_scalar) for t in range(TAPS)]
+        keep_clock(1)
         psig0_mx = quantise("psig0", psig_g, 2 * P)
+        sig_g = turn_taps("sig0", sig_rows[0], (by_scalar, by_vector))
+        keep_clock(1)
         x_grouped = stage.tile([P, TAPS, B, DIL, 2, 2], BF16, align_bytes=64)
         x_by_time = x_sb[:].rearrange("p (b h v) t -> p b t v h", b=B, h=2)
         for tap in range(TAPS):
@@ -177,63 +185,88 @@ def tile_gatedresidualcondconv_pa_s_kernel(
         x_mx = quantise("x", x_grouped[:].rearrange("p h b t v j -> p (h b t v j)"), TAPS * N)
         sig0_mx.append(quantise("sig01", sig_g[1], 2 * P))
 
-        pgate_g = turn_plain("pgate0", pgate_rows[0], 2, by_vector)
+        pgate_g = turn_plain("pgate0", pgate_rows[0], 2, by_scalar)
         bias_bank = turned.tile([P, P], F32, tag="bank")
         nc.tensor.transpose(bias_bank[:], bias_rows[:], ident[:])
-        gate_g = [turn_tap("gate0%d" % t, gate_rows[0], t, by_scalar) for t in range(TAPS)]
         bias = const.tile([P, 2, PACK], BF16)
         nc.vector.tensor_copy(
             out=bias[:].rearrange("p g s -> p (g s)").bitcast(F32), in_=bias_bank[:, 0 : 2 * HALVES]
         )
+        pgate0_mx = quantise("pgate0", pgate_g, 2 * P)
+
+        gate_g = turn_taps("gate0", gate_rows[0], (by_scalar, by_vector))
+        keep_clock(2)
         c_grouped = stage.tile([P, B, DIL, PACK], BF16, align_bytes=64)
         c_by_time = c_sb[:].rearrange("p (b u) (e t) -> p b t (u e)", b=B, e=2)
         nc.vector.tensor_copy(out=c_grouped[:], in_=c_by_time[:, :, DIL:T, :])
-        pgate0_mx = quantise("pgate0", pgate_g, 2 * P)
         gate0_mx = [quantise("gate00", gate_g[0], 2 * P)]
         c_mx = quantise("c", c_grouped[:].rearrange("p b t s -> p (b t s)"), N)
         gate0_mx.append(quantise("gate01", gate_g[1], 2 * P))
 
+        sig_g = turn_taps("sig1", sig_rows[1], (by_scalar, by_vector))
         psig_g = turn_plain("psig1", psig_rows[1], 2, by_scalar)
-        sig_g = [turn_tap("sig1%d" % t, sig_rows[1], t, by_scalar) for t in range(TAPS)]
         branch(0, 0, sig0_mx, psig0_mx)
-        psig1_mx = quantise("psig1", psig_g, 2 * P)
-        sig1_mx = [quantise("sig10", sig_g[0], 2 * P)]
-
-        pgate_g = turn_plain("pgate1", pgate_rows[1], 2, by_vector)
-        sig1_mx.append(quantise("sig11", sig_g[1], 2 * P))
-        gate_g = [turn_tap("gate1%d" % t, gate_rows[1], t, by_scalar) for t in range(TAPS)]
         branch(1, 0, gate0_mx, pgate0_mx)
-        pgate1_mx = quantise("pgate1", pgate_g, 2 * P)
-        gate1_mx = [quantise("gate1%d" % t, gate_g[t], 2 * P) for t in range(TAPS)]
-        branch(0, 1, sig1_mx, psig1_mx)
+        sig1_mx = [quantise("sig10", sig_g[0], 2 * P)]
+        psig1_mx = quantise("psig1", psig_g, 2 * P)
+        sig1_mx.append(quantise("sig11", sig_g[1], 2 * P))
 
-        res_g = [turn_plain("res%d" % h, res_rows[h], 2, (by_scalar, by_vector)[h]) for h in range(2)]
-        branch(1, 1, gate1_mx, pgate1_mx)
+        gate_g = turn_taps("gate1", gate_rows[1], (by_scalar, by_vector))
+        pgate_g = turn_plain("pgate1", pgate_rows[1], 2, by_scalar)
+        branch(0, 1, sig1_mx, psig1_mx)
+        gate1_mx = [quantise("gate1%d" % t, gate_g[t], 2 * P) for t in range(TAPS)]
+        pgate1_mx = quantise("pgate1", pgate_g, 2 * P)
+
+        res_g = [turn_plain("res%d" % h, res_rows[h], 2, (by_vector, by_scalar)[h]) for h in range(2)]
+
+        accs = [sums.tile([P, N], F32, tag="sum", name="acc11%d" % e) for e in range(2)]
+        for e in range(2):
+            for t in range(TAPS):
+                mx_pass(accs[e][:], gate1_mx[t], e * P, x_mx, t * N, t == 0, False)
+        for e in range(2):
+            mx_pass(accs[e][:], pgate1_mx, e * P, c_mx, 0, False, True)
+        gate_acts(1, 1, [accs[e][:] for e in range(2)])
+
         skp_g = turn_plain("skp", skp_rows, 1, by_scalar)
-        res_mx = [quantise("res%d" % h, res_g[h], 2 * P) for h in range(2)]
+        keep_clock(4)
+        res_mx = [None, quantise("res1", res_g[1], 2 * P)]
+        res_mx[0] = quantise("res0", res_g[0], 2 * P)
+
+        z_grouped = stage.tile([P, B, DIL, PACK], BF16, align_bytes=64)
+        z_codes = mx.tile([P, N], U32, align_bytes=64)
+        z_scales = mx.tile([P, N], U8, align_bytes=64)
+        for b in range(B):
+            times = slice(b * DIL, (b + 1) * DIL)
+            nc.vector.tensor_tensor(
+                out=z_grouped[:, b],
+                in0=tanh_filt[:, :, times].rearrange("p s n -> p n s"),
+                in1=sigm_gate[:, :, times].rearrange("p s n -> p n s"),
+                op=ALU.mult,
+            )
+        for b in range(B):
+            times = slice(b * DIL, (b + 1) * DIL)
+            nc.vector.quantize_mx(
+                out=z_codes[:, times].bitcast(FP8X4),
+                scales=z_scales[:, times],
+                in_=z_grouped[:, b].rearrange("p n s -> p (n s)"),
+            )
         skp_mx = quantise("skp", skp_g, P)
 
-        z_grouped = stage.tile([P, N, PACK], BF16, align_bytes=64)
-        nc.vector.tensor_tensor(
-            out=z_grouped[:],
-            in0=tanh_filt[:].rearrange("p s n -> p n s"),
-            in1=sigm_gate[:].rearrange("p s n -> p n s"),
-            op=ALU.mult,
-        )
-        z_mx = quantise("z", z_grouped[:].rearrange("p n s -> p (n s)"), N)
-
-        res_sum = sums.tile([P, PACK, B, DIL], F32, tag="sum")
-        for j in range(PACK):
-            mx_pass(res_sum[:, j].rearrange("p b t -> p (b t)"), res_mx[j // 2], (j % 2) * P, z_mx, 0, True, True)
+        res_sums = [sums.tile([P, PACK, DIL], F32, tag="sum", name="res_sum%d" % b) for b in range(B)]
+        for b in range(B):
+            for j in range(PACK):
+                mx_pass(res_sums[b][:, j, :], res_mx[j // 2], (j % 2) * P, (z_codes, z_scales), b * DIL, True, True, DIL)
         skp_sum = sums.tile([P, N], F32, tag="sum")
-        mx_pass(skp_sum[:], skp_mx, 0, z_mx, 0, True, True)
-
-        skp_sb = stage.tile([P, B, DIL], F32)
-        nc.scalar.copy(out=skp_sb[:].rearrange("p b t -> p (b t)"), in_=skp_sum[:])
-        nc.sync.dma_start(out=out_1.rearrange("b s t -> s b t"), in_=skp_sb[:])
+        mx_pass(skp_sum[:], skp_mx, 0, (z_codes, z_scales), 0, True, True)
 
         x_later = x_res[:].rearrange("p b (j t) -> p b j t", j=PACK)[:, :, :, DIL:T]
         sig_sb = stage.tile([P, B, PACK, DIL], F32)
         for b in range(B):
-            nc.vector.tensor_tensor(out=sig_sb[:, b], in0=res_sum[:, :, b, :], in1=x_later[:, b], op=ALU.add)
-            nc.sync.dma_start(out=out_0[b].rearrange("(p j) t -> p (j t)", j=PACK), in_=sig_sb[:, b].rearrange("p j t -> p (j t)"))
+            nc.vector.tensor_tensor(out=sig_sb[:, b], in0=res_sums[b][:], in1=x_later[:, b], op=ALU.add)
+            nc.sync.dma_start(
+                out=out_0[b].rearrange("(p j) t -> p (j t)", j=PACK), in_=sig_sb[:, b].rearrange("p j t -> p (j t)")
+            )
+
+        skp_sb = stage.tile([P, B, DIL], F32)
+        nc.scalar.copy(out=skp_sb[:].rearrange("p b t -> p (b t)"), in_=skp_sum[:])
+        nc.scalar.dma_start(out=out_1.rearrange("b s t -> s b t"), in_=skp_sb[:])

@@ -42,13 +42,13 @@ def tile_gatedresidualcondconv_pa_s_kernel(
 
         zeros = const.tile([P, P], F32)
         nc.vector.memset(zeros[:], 0.0)
-        spare = spare_pool.tile([P, P], F32)
+        spare = spare_pool.tile([P, TAPS * N], F32)
 
         def keep_clock(times):
             for i in range(times):
-                nc.tensor.matmul(spare[:], lhsT=zeros[:], rhs=zeros[:], start=True, stop=True)
+                nc.tensor.matmul(spare[:, 0:P], lhsT=zeros[:], rhs=zeros[:], start=True, stop=True)
 
-        keep_clock(3)
+        keep_clock(4)
 
         ident = const.tile([P, P], F32)
         make_identity(nc, ident[:])
@@ -176,7 +176,7 @@ def tile_gatedresidualcondconv_pa_s_kernel(
         keep_clock(1)
         psig0_mx = quantise("psig0", psig_g, 2 * P)
         sig_g = turn_taps("sig0", sig_rows[0], (by_scalar, by_vector))
-        keep_clock(1)
+        keep_clock(2)
         x_grouped = stage.tile([P, TAPS, B, DIL, 2, 2], BF16, align_bytes=64)
         x_by_time = x_sb[:].rearrange("p (b h v) t -> p b t v h", b=B, h=2)
         for tap in range(TAPS):
@@ -188,6 +188,7 @@ def tile_gatedresidualcondconv_pa_s_kernel(
         pgate_g = turn_plain("pgate0", pgate_rows[0], 2, by_scalar)
         bias_bank = turned.tile([P, P], F32, tag="bank")
         nc.tensor.transpose(bias_bank[:], bias_rows[:], ident[:])
+        keep_clock(1)
         bias = const.tile([P, 2, PACK], BF16)
         nc.vector.tensor_copy(
             out=bias[:].rearrange("p g s -> p (g s)").bitcast(F32), in_=bias_bank[:, 0 : 2 * HALVES]
@@ -204,6 +205,7 @@ def tile_gatedresidualcondconv_pa_s_kernel(
         gate0_mx.append(quantise("gate01", gate_g[1], 2 * P))
 
         sig_g = turn_taps("sig1", sig_rows[1], (by_scalar, by_vector))
+        keep_clock(1)
         psig_g = turn_plain("psig1", psig_rows[1], 2, by_scalar)
         branch(0, 0, sig0_mx, psig0_mx)
         branch(1, 0, gate0_mx, pgate0_mx)
@@ -228,7 +230,8 @@ def tile_gatedresidualcondconv_pa_s_kernel(
         gate_acts(1, 1, [accs[e][:] for e in range(2)])
 
         skp_g = turn_plain("skp", skp_rows, 1, by_scalar)
-        keep_clock(4)
+        for i in range(6):
+            mx_pass(spare[:], x_mx, 0, x_mx, 0, True, True, TAPS * N)
         res_mx = [None, quantise("res1", res_g[1], 2 * P)]
         res_mx[0] = quantise("res0", res_g[0], 2 * P)
 

@@ -20,7 +20,6 @@ T = 128
 DIL = 64
 TAPS = 2
 N = B * DIL
-GROUPS = 4
 HALVES = 2
 
 FLOPS = 2 * N * (6 * CH * CH + CH * CH + SKIP * CH)
@@ -35,18 +34,17 @@ def tile_gatedresidualcondconv_pa_s_kernel(
         raw = ctx.enter_context(tc.tile_pool(name="raw", bufs=1))
         stage = ctx.enter_context(tc.tile_pool(name="stage", bufs=1))
         mx = ctx.enter_context(tc.tile_pool(name="mx", bufs=1))
-        turned = ctx.enter_context(tc.psum_pool(name="turned", bufs=4))
-        spare_pool = ctx.enter_context(tc.psum_pool(name="spare", bufs=1))
+        turned = ctx.enter_context(tc.psum_pool(name="turned", bufs=5))
         sums = ctx.enter_context(tc.psum_pool(name="sums", bufs=3))
         ctx.enter_context(tc.manual_schedule())
 
         zeros = const.tile([P, P], F32)
         nc.vector.memset(zeros[:], 0.0)
-        spare = spare_pool.tile([P, TAPS * N], F32)
+        spare = sums.tile([P, P], F32, tag="sum", name="spare")
 
         def keep_clock(times):
             for i in range(times):
-                nc.tensor.matmul(spare[:, 0:P], lhsT=zeros[:], rhs=zeros[:], start=True, stop=True)
+                nc.tensor.matmul(spare[:], lhsT=zeros[:], rhs=zeros[:], start=True, stop=True)
 
         keep_clock(4)
 
@@ -58,43 +56,41 @@ def tile_gatedresidualcondconv_pa_s_kernel(
 
         bias_rows = const.tile([P, P], F32)
         nc.vector.memset(bias_rows[:], 0.0)
-        ident_bf = const.tile([P, P], BF16)
-        nc.vector.tensor_copy(out=ident_bf[:], in_=ident[:])
 
         def load(name, shape, view):
             rows = raw.tile(shape, BF16, name=name)
             nc.sync.dma_start(out=rows[:], in_=view)
             return rows
 
-        sig_view = w_sig.rearrange("(u g d) (h r) t -> u (d h) g (r t)", u=HALVES, g=GROUPS, h=2)
-        gate_view = w_gate.rearrange("(u g d) (h r) t -> u (d h) g (r t)", u=HALVES, g=GROUPS, h=2)
+        sig_view = w_sig.rearrange("(u p e) r t -> p u e (r t)", u=HALVES, e=2)
+        gate_view = w_gate.rearrange("(u p e) r t -> p u e (r t)", u=HALVES, e=2)
         psig_view = w_psig.rearrange("(u p e) c -> p u e c", u=HALVES, e=2)
         pgate_view = w_pgate.rearrange("(u p e) c -> p u e c", u=HALVES, e=2)
         res_view = w_res.rearrange("(p h i) d -> p h i d", h=2, i=2)
 
         def load_taps(name, view):
-            return [load("%s_%d" % (name, b), [P, 2, CH], view[:, 2 * b : 2 * b + 2, :]) for b in range(2)]
+            return [load("%s_%d" % (name, e), [P, TAPS * CH], view[:, e, :]) for e in range(2)]
 
         sig_rows = [None] * HALVES
         gate_rows = [None] * HALVES
         psig_rows = [None] * HALVES
         pgate_rows = [None] * HALVES
         psig_rows[0] = load("psig0", [P, 2, CH], psig_view[:, 0])
-        sig_rows[0] = load_taps("sig0", sig_view[0])
-        x_sb = load("x_sb", [P, B * PACK, T], x.rearrange("b (h v p) t -> p (b h v) t", h=2, p=P))
+        sig_rows[0] = load_taps("sig0", sig_view[:, 0])
+        x_sb = load("x_sb", [P, B * PACK, T], x.rearrange("b (j p) t -> p (b j) t", p=P))
         pgate_rows[0] = load("pgate0", [P, 2, CH], pgate_view[:, 0])
         for g, b_vec in enumerate((b_sig, b_gate)):
             nc.sync.dma_start(
                 out=bias_rows[g * HALVES : (g + 1) * HALVES, :].bitcast(BF16),
                 in_=b_vec.rearrange("(u w) -> u w", u=HALVES),
             )
-        gate_rows[0] = load_taps("gate0", gate_view[0])
+        gate_rows[0] = load_taps("gate0", gate_view[:, 0])
         c_sb = load(
             "c_sb", [P, B * HALVES, 2 * T], cond.rearrange("b (u p e) t -> p (b u) (e t)", u=HALVES, e=2)
         )
-        sig_rows[1] = load_taps("sig1", sig_view[1])
+        sig_rows[1] = load_taps("sig1", sig_view[:, 1])
         psig_rows[1] = load("psig1", [P, 2, CH], psig_view[:, 1])
-        gate_rows[1] = load_taps("gate1", gate_view[1])
+        gate_rows[1] = load_taps("gate1", gate_view[:, 1])
         pgate_rows[1] = load("pgate1", [P, 2, CH], pgate_view[:, 1])
         res_rows = [load("res%d" % h, [P, 2, CH], res_view[:, h]) for h in range(2)]
         skp_rows = load("skp", [P, 1, CH], w_skp.rearrange("s (o d) -> s o d", o=1))
@@ -107,22 +103,15 @@ def tile_gatedresidualcondconv_pa_s_kernel(
             return codes, scales
 
         def turn_taps(name, rows, empty_banks):
-            banks = [turned.tile([P, 2, GROUPS, P], BF16, tag="bank", name="%s%d_bank" % (name, t)) for t in range(TAPS)]
-            for half in range(2):
-                for tap in range(TAPS):
-                    for g in range(2):
-                        for v in range(2):
-                            nc.tensor.transpose(
-                                banks[tap][:, v, 2 * half + g, :],
-                                rows[half][:, g, 2 * P * v + tap : 2 * P * (v + 1) : TAPS],
-                                ident_bf[:],
-                            )
             flat = []
-            for tap in range(TAPS):
-                grouped = stage.tile([P, 2, P, PACK], BF16, name="%s%d_grouped" % (name, tap), align_bytes=64)
-                words = banks[tap][:].rearrange("p v g i -> p (v g i)").bitcast(F32)
-                empty_banks[tap](out=grouped[:].bitcast(F32), in_=words.rearrange("p (v m e) -> p e m v", v=2, e=2))
-                flat.append(grouped[:].rearrange("p e m s -> p (e m s)"))
+            for e in range(2):
+                words = rows[e][:].bitcast(F32)
+                bank = turned.tile([P, PACK, P], F32, tag="bank", name="%s%d_bank" % (name, e))
+                for j in range(PACK):
+                    nc.tensor.transpose(bank[:, j, :], words[:, j * P : (j + 1) * P], ident[:])
+                grouped = stage.tile([P, TAPS, P, PACK], BF16, name="%s%d_grouped" % (name, e), align_bytes=64)
+                empty_banks[e](out=grouped[:], in_=bank[:].bitcast(BF16).rearrange("p j (m t) -> p t m j", t=TAPS))
+                flat.append(grouped[:].rearrange("p t m j -> p (t m j)"))
             return flat
 
         def turn_plain(name, rows, chunks, empty_bank):
@@ -135,15 +124,15 @@ def tile_gatedresidualcondconv_pa_s_kernel(
             empty_bank(out=grouped[:].bitcast(F32), in_=bank[:].rearrange("p i v m -> p i m v"))
             return grouped[:].rearrange("p i m t -> p (i m t)")
 
-        def mx_pass(out, weights, first, moving, moving_first, start, stop, columns=N):
+        def mx_pass(out, weights, first, moving, moving_first, start, stop):
             w_codes, w_scales = weights
             m_codes, m_scales = moving
             nc.tensor.matmul_mx(
                 out=out,
                 lhsT=w_codes[:, first : first + P].bitcast(FP8X4),
                 lhsT_scale=w_scales[:, first : first + P],
-                rhs=m_codes[:, moving_first : moving_first + columns].bitcast(FP8X4),
-                rhs_scale=m_scales[:, moving_first : moving_first + columns],
+                rhs=m_codes[:, moving_first : moving_first + N].bitcast(FP8X4),
+                rhs_scale=m_scales[:, moving_first : moving_first + N],
                 start=start,
                 stop=stop,
             )
@@ -164,8 +153,8 @@ def tile_gatedresidualcondconv_pa_s_kernel(
         def branch(g, u, taps_mx, proj_mx):
             acc = sums.tile([P, 2, N], F32, tag="sum", name="acc%d%d" % (g, u))
             for e in range(2):
-                mx_pass(acc[:, e, :], taps_mx[0], e * P, x_mx, 0, True, False)
-                mx_pass(acc[:, e, :], taps_mx[1], e * P, x_mx, N, False, False)
+                mx_pass(acc[:, e, :], taps_mx[e], 0, x_mx, 0, True, False)
+                mx_pass(acc[:, e, :], taps_mx[e], P, x_mx, N, False, False)
                 mx_pass(acc[:, e, :], proj_mx, e * P, c_mx, 0, False, True)
             gate_acts(g, u, [acc[:, e, :] for e in range(2)])
 
@@ -175,15 +164,15 @@ def tile_gatedresidualcondconv_pa_s_kernel(
         psig_g = turn_plain("psig0", psig_rows[0], 2, by_scalar)
         keep_clock(1)
         psig0_mx = quantise("psig0", psig_g, 2 * P)
-        sig_g = turn_taps("sig0", sig_rows[0], (by_scalar, by_vector))
+        sig_g = turn_taps("sig0", sig_rows[0], (by_scalar, by_scalar))
         keep_clock(2)
-        x_grouped = stage.tile([P, TAPS, B, DIL, 2, 2], BF16, align_bytes=64)
-        x_by_time = x_sb[:].rearrange("p (b h v) t -> p b t v h", b=B, h=2)
+        x_grouped = stage.tile([P, TAPS, B, DIL, PACK], BF16, align_bytes=64)
+        x_by_time = x_sb[:].rearrange("p (b j) t -> p b t j", b=B)
         for tap in range(TAPS):
             nc.vector.tensor_copy(out=x_grouped[:, tap], in_=x_by_time[:, :, tap * DIL : (tap + 1) * DIL])
-        sig0_mx = [quantise("sig00", sig_g[0], 2 * P)]
-        x_mx = quantise("x", x_grouped[:].rearrange("p h b t v j -> p (h b t v j)"), TAPS * N)
-        sig0_mx.append(quantise("sig01", sig_g[1], 2 * P))
+        sig0_mx = [quantise("sig00", sig_g[0], TAPS * P)]
+        x_mx = quantise("x", x_grouped[:].rearrange("p h b t j -> p (h b t j)"), TAPS * N)
+        sig0_mx.append(quantise("sig01", sig_g[1], TAPS * P))
 
         pgate_g = turn_plain("pgate0", pgate_rows[0], 2, by_scalar)
         bias_bank = turned.tile([P, P], F32, tag="bank")
@@ -200,9 +189,8 @@ def tile_gatedresidualcondconv_pa_s_kernel(
         c_grouped = stage.tile([P, B, DIL, PACK], BF16, align_bytes=64)
         c_by_time = c_sb[:].rearrange("p (b u) (e t) -> p b t (u e)", b=B, e=2)
         nc.vector.tensor_copy(out=c_grouped[:], in_=c_by_time[:, :, DIL:T, :])
-        gate0_mx = [quantise("gate00", gate_g[0], 2 * P)]
+        gate0_mx = [quantise("gate0%d" % e, gate_g[e], TAPS * P) for e in range(2)]
         c_mx = quantise("c", c_grouped[:].rearrange("p b t s -> p (b t s)"), N)
-        gate0_mx.append(quantise("gate01", gate_g[1], 2 * P))
 
         sig_g = turn_taps("sig1", sig_rows[1], (by_scalar, by_vector))
         keep_clock(1)
@@ -216,7 +204,7 @@ def tile_gatedresidualcondconv_pa_s_kernel(
         gate_g = turn_taps("gate1", gate_rows[1], (by_scalar, by_vector))
         pgate_g = turn_plain("pgate1", pgate_rows[1], 2, by_scalar)
         branch(0, 1, sig1_mx, psig1_mx)
-        gate1_mx = [quantise("gate1%d" % t, gate_g[t], 2 * P) for t in range(TAPS)]
+        gate1_mx = [quantise("gate1%d" % e, gate_g[e], TAPS * P) for e in range(2)]
         pgate1_mx = quantise("pgate1", pgate_g, 2 * P)
 
         res_g = [turn_plain("res%d" % h, res_rows[h], 2, (by_vector, by_scalar)[h]) for h in range(2)]
@@ -224,52 +212,39 @@ def tile_gatedresidualcondconv_pa_s_kernel(
         accs = [sums.tile([P, N], F32, tag="sum", name="acc11%d" % e) for e in range(2)]
         for e in range(2):
             for t in range(TAPS):
-                mx_pass(accs[e][:], gate1_mx[t], e * P, x_mx, t * N, t == 0, False)
+                mx_pass(accs[e][:], gate1_mx[e], t * P, x_mx, t * N, t == 0, False)
         for e in range(2):
             mx_pass(accs[e][:], pgate1_mx, e * P, c_mx, 0, False, True)
         gate_acts(1, 1, [accs[e][:] for e in range(2)])
 
         skp_g = turn_plain("skp", skp_rows, 1, by_scalar)
-        for i in range(6):
-            mx_pass(spare[:], x_mx, 0, x_mx, 0, True, True, TAPS * N)
         res_mx = [None, quantise("res1", res_g[1], 2 * P)]
         res_mx[0] = quantise("res0", res_g[0], 2 * P)
 
-        z_grouped = stage.tile([P, B, DIL, PACK], BF16, align_bytes=64)
-        z_codes = mx.tile([P, N], U32, align_bytes=64)
-        z_scales = mx.tile([P, N], U8, align_bytes=64)
-        for b in range(B):
-            times = slice(b * DIL, (b + 1) * DIL)
-            nc.vector.tensor_tensor(
-                out=z_grouped[:, b],
-                in0=tanh_filt[:, :, times].rearrange("p s n -> p n s"),
-                in1=sigm_gate[:, :, times].rearrange("p s n -> p n s"),
-                op=ALU.mult,
-            )
-        for b in range(B):
-            times = slice(b * DIL, (b + 1) * DIL)
-            nc.vector.quantize_mx(
-                out=z_codes[:, times].bitcast(FP8X4),
-                scales=z_scales[:, times],
-                in_=z_grouped[:, b].rearrange("p n s -> p (n s)"),
-            )
+        z_grouped = stage.tile([P, N, PACK], BF16, align_bytes=64)
+        nc.vector.tensor_tensor(
+            out=z_grouped[:],
+            in0=tanh_filt[:].rearrange("p s n -> p n s"),
+            in1=sigm_gate[:].rearrange("p s n -> p n s"),
+            op=ALU.mult,
+        )
+        z_mx = quantise("z", z_grouped[:].rearrange("p n s -> p (n s)"), N)
         skp_mx = quantise("skp", skp_g, P)
 
-        res_sums = [sums.tile([P, PACK, DIL], F32, tag="sum", name="res_sum%d" % b) for b in range(B)]
-        for b in range(B):
-            for j in range(PACK):
-                mx_pass(res_sums[b][:, j, :], res_mx[j // 2], (j % 2) * P, (z_codes, z_scales), b * DIL, True, True, DIL)
+        res_sum = sums.tile([P, PACK, B, DIL], F32, tag="sum")
+        for j in range(PACK):
+            mx_pass(res_sum[:, j].rearrange("p b t -> p (b t)"), res_mx[j // 2], (j % 2) * P, z_mx, 0, True, True)
         skp_sum = sums.tile([P, N], F32, tag="sum")
-        mx_pass(skp_sum[:], skp_mx, 0, (z_codes, z_scales), 0, True, True)
+        mx_pass(skp_sum[:], skp_mx, 0, z_mx, 0, True, True)
+
+        skp_sb = stage.tile([P, B, DIL], F32)
+        nc.scalar.copy(out=skp_sb[:].rearrange("p b t -> p (b t)"), in_=skp_sum[:])
+        nc.sync.dma_start(out=out_1.rearrange("b s t -> s b t"), in_=skp_sb[:])
 
         x_later = x_res[:].rearrange("p b (j t) -> p b j t", j=PACK)[:, :, :, DIL:T]
         sig_sb = stage.tile([P, B, PACK, DIL], F32)
         for b in range(B):
-            nc.vector.tensor_tensor(out=sig_sb[:, b], in0=res_sums[b][:], in1=x_later[:, b], op=ALU.add)
+            nc.vector.tensor_tensor(out=sig_sb[:, b], in0=res_sum[:, :, b, :], in1=x_later[:, b], op=ALU.add)
             nc.sync.dma_start(
                 out=out_0[b].rearrange("(p j) t -> p (j t)", j=PACK), in_=sig_sb[:, b].rearrange("p j t -> p (j t)")
             )
-
-        skp_sb = stage.tile([P, B, DIL], F32)
-        nc.scalar.copy(out=skp_sb[:].rearrange("p b t -> p (b t)"), in_=skp_sum[:])
-        nc.scalar.dma_start(out=out_1.rearrange("b s t -> s b t"), in_=skp_sb[:])

@@ -174,7 +174,7 @@ def tile_gatedresidualcondconv_pa_s_kernel(
         x_mx = quantise("x", x_grouped[:].rearrange("p h b t j -> p (h b t j)"), TAPS * N)
         sig0_mx.append(quantise("sig01", sig_g[1], TAPS * P))
 
-        pgate_g = turn_plain("pgate0", pgate_rows[0], 2, by_scalar)
+        pgate_g = turn_plain("pgate0", pgate_rows[0], 2, by_vector)
         bias_bank = turned.tile([P, P], F32, tag="bank")
         nc.tensor.transpose(bias_bank[:], bias_rows[:], ident[:])
         keep_clock(1)
@@ -182,27 +182,28 @@ def tile_gatedresidualcondconv_pa_s_kernel(
         nc.vector.tensor_copy(
             out=bias[:].rearrange("p g s -> p (g s)").bitcast(F32), in_=bias_bank[:, 0 : 2 * HALVES]
         )
-        pgate0_mx = quantise("pgate0", pgate_g, 2 * P)
 
-        gate_g = turn_taps("gate0", gate_rows[0], (by_scalar, by_vector))
+        gate_g = turn_taps("gate0", gate_rows[0], (by_scalar, by_scalar))
         keep_clock(2)
         c_grouped = stage.tile([P, B, DIL, PACK], BF16, align_bytes=64)
         c_by_time = c_sb[:].rearrange("p (b u) (e t) -> p b t (u e)", b=B, e=2)
         nc.vector.tensor_copy(out=c_grouped[:], in_=c_by_time[:, :, DIL:T, :])
-        gate0_mx = [quantise("gate0%d" % e, gate_g[e], TAPS * P) for e in range(2)]
+        pgate0_mx = quantise("pgate0", pgate_g, 2 * P)
+        gate0_mx = [quantise("gate00", gate_g[0], TAPS * P)]
         c_mx = quantise("c", c_grouped[:].rearrange("p b t s -> p (b t s)"), N)
+        gate0_mx.append(quantise("gate01", gate_g[1], TAPS * P))
 
         sig_g = turn_taps("sig1", sig_rows[1], (by_scalar, by_vector))
         keep_clock(1)
         psig_g = turn_plain("psig1", psig_rows[1], 2, by_scalar)
         branch(0, 0, sig0_mx, psig0_mx)
-        branch(1, 0, gate0_mx, pgate0_mx)
         sig1_mx = [quantise("sig10", sig_g[0], 2 * P)]
         psig1_mx = quantise("psig1", psig_g, 2 * P)
         sig1_mx.append(quantise("sig11", sig_g[1], 2 * P))
 
         gate_g = turn_taps("gate1", gate_rows[1], (by_scalar, by_vector))
         pgate_g = turn_plain("pgate1", pgate_rows[1], 2, by_scalar)
+        branch(1, 0, gate0_mx, pgate0_mx)
         branch(0, 1, sig1_mx, psig1_mx)
         gate1_mx = [quantise("gate1%d" % e, gate_g[e], TAPS * P) for e in range(2)]
         pgate1_mx = quantise("pgate1", pgate_g, 2 * P)
@@ -219,7 +220,6 @@ def tile_gatedresidualcondconv_pa_s_kernel(
 
         skp_g = turn_plain("skp", skp_rows, 1, by_scalar)
         res_mx = [None, quantise("res1", res_g[1], 2 * P)]
-        res_mx[0] = quantise("res0", res_g[0], 2 * P)
 
         z_grouped = stage.tile([P, N, PACK], BF16, align_bytes=64)
         nc.vector.tensor_tensor(
@@ -228,6 +228,7 @@ def tile_gatedresidualcondconv_pa_s_kernel(
             in1=sigm_gate[:].rearrange("p s n -> p n s"),
             op=ALU.mult,
         )
+        res_mx[0] = quantise("res0", res_g[0], 2 * P)
         z_mx = quantise("z", z_grouped[:].rearrange("p n s -> p (n s)"), N)
         skp_mx = quantise("skp", skp_g, P)
 

@@ -40,11 +40,11 @@ def tile_gatedresidualcondconv_pa_s_kernel(
 
         zeros = const.tile([P, P], F32)
         nc.vector.memset(zeros[:], 0.0)
-        spare = sums.tile([P, P], F32, tag="sum", name="spare")
+        spare = sums.tile([P, TAPS * N], F32, tag="sum", name="spare")
 
         def keep_clock(times):
             for i in range(times):
-                nc.tensor.matmul(spare[:], lhsT=zeros[:], rhs=zeros[:], start=True, stop=True)
+                nc.tensor.matmul(spare[:, 0:P], lhsT=zeros[:], rhs=zeros[:], start=True, stop=True)
 
         keep_clock(4)
 
@@ -124,18 +124,22 @@ def tile_gatedresidualcondconv_pa_s_kernel(
             empty_bank(out=grouped[:].bitcast(F32), in_=bank[:].rearrange("p i v m -> p i m v"))
             return grouped[:].rearrange("p i m t -> p (i m t)")
 
-        def mx_pass(out, weights, first, moving, moving_first, start, stop):
+        def mx_pass(out, weights, first, moving, moving_first, start, stop, columns=N):
             w_codes, w_scales = weights
             m_codes, m_scales = moving
             nc.tensor.matmul_mx(
                 out=out,
                 lhsT=w_codes[:, first : first + P].bitcast(FP8X4),
                 lhsT_scale=w_scales[:, first : first + P],
-                rhs=m_codes[:, moving_first : moving_first + N].bitcast(FP8X4),
-                rhs_scale=m_scales[:, moving_first : moving_first + N],
+                rhs=m_codes[:, moving_first : moving_first + columns].bitcast(FP8X4),
+                rhs_scale=m_scales[:, moving_first : moving_first + columns],
                 start=start,
                 stop=stop,
             )
+
+        def keep_clock_mx(times, spare_sum):
+            for i in range(times):
+                mx_pass(spare_sum[:], x_mx, 0, x_mx, 0, True, True, TAPS * N)
 
         tanh_filt = stage.tile([P, PACK, N], F32)
         sigm_gate = stage.tile([P, PACK, N], F32)
@@ -165,7 +169,7 @@ def tile_gatedresidualcondconv_pa_s_kernel(
         keep_clock(1)
         psig0_mx = quantise("psig0", psig_g, 2 * P)
         sig_g = turn_taps("sig0", sig_rows[0], (by_scalar, by_scalar))
-        keep_clock(2)
+        keep_clock(3)
         x_grouped = stage.tile([P, TAPS, B, DIL, PACK], BF16, align_bytes=64)
         x_by_time = x_sb[:].rearrange("p (b j) t -> p b t j", b=B)
         for tap in range(TAPS):
@@ -184,7 +188,8 @@ def tile_gatedresidualcondconv_pa_s_kernel(
         )
 
         gate_g = turn_taps("gate0", gate_rows[0], (by_scalar, by_scalar))
-        keep_clock(2)
+        keep_clock(1)
+        keep_clock_mx(3, spare)
         c_grouped = stage.tile([P, B, DIL, PACK], BF16, align_bytes=64)
         c_by_time = c_sb[:].rearrange("p (b u) (e t) -> p b t (u e)", b=B, e=2)
         nc.vector.tensor_copy(out=c_grouped[:], in_=c_by_time[:, :, DIL:T, :])
@@ -219,6 +224,7 @@ def tile_gatedresidualcondconv_pa_s_kernel(
         gate_acts(1, 1, [accs[e][:] for e in range(2)])
 
         skp_g = turn_plain("skp", skp_rows, 1, by_scalar)
+        keep_clock_mx(4, sums.tile([P, TAPS * N], F32, tag="sum", name="spare_late"))
         res_mx = [None, quantise("res1", res_g[1], 2 * P)]
 
         z_grouped = stage.tile([P, N, PACK], BF16, align_bytes=64)

from contextlib import ExitStack

import concourse.mybir as mybir
from concourse.masks import make_identity

F32 = mybir.dt.float32
BF16 = mybir.dt.bfloat16
U32 = mybir.dt.uint32
U8 = mybir.dt.uint8
FP8X4 = mybir.dt.float8_e4m3fn_x4
ACT = mybir.ActivationFunctionType
ALU = mybir.AluOpType

P = 128
PACK = 4
B = 2
CH = 512
SKIP = 128
T = 128
DIL = 64
TAPS = 2
N = B * DIL
HALVES = 2

FLOPS = 2 * N * (6 * CH * CH + CH * CH + SKIP * CH)


def tile_gatedresidualcondconv_pa_s_kernel(
    tc, x, cond, w_sig, b_sig, w_gate, b_gate, w_psig, w_pgate, w_res, w_skp, out_0, out_1
):
    nc = tc.nc
    with ExitStack() as ctx:
        const = ctx.enter_context(tc.tile_pool(name="const", bufs=1))
        raw = ctx.enter_context(tc.tile_pool(name="raw", bufs=1))
        stage = ctx.enter_context(tc.tile_pool(name="stage", bufs=1))
        mx = ctx.enter_context(tc.tile_pool(name="mx", bufs=1))
        turned = ctx.enter_context(tc.psum_pool(name="turned", bufs=5))
        sums = ctx.enter_context(tc.psum_pool(name="sums", bufs=3))
        ctx.enter_context(tc.manual_schedule())

        zeros = const.tile([P, P], F32)
        nc.vector.memset(zeros[:], 0.0)
        spare = sums.tile([P, TAPS * N], F32, tag="sum", name="spare")

        def keep_clock(times):
            for i in range(times):
                nc.tensor.matmul(spare[:, 0:P], lhsT=zeros[:], rhs=zeros[:], start=True, stop=True)

        keep_clock(4)

        ident = const.tile([P, P], F32)
        make_identity(nc, ident[:])
        warm = const.tile([P, 1], F32)
        nc.vector.memset(warm[:], 0.0)
        nc.scalar.activation(out=warm[:], in_=warm[:], func=ACT.Sigmoid)

        bias_rows = const.tile([P, P], F32)
        nc.vector.memset(bias_rows[:], 0.0)

        def load(name, shape, view):
            rows = raw.tile(shape, BF16, name=name)
            nc.sync.dma_start(out=rows[:], in_=view)
            return rows

        sig_view = w_sig.rearrange("(u p e) r t -> p u e (r t)", u=HALVES, e=2)
        gate_view = w_gate.rearrange("(u p e) r t -> p u e (r t)", u=HALVES, e=2)
        psig_view = w_psig.rearrange("(u p e) c -> p u e c", u=HALVES, e=2)
        pgate_view = w_pgate.rearrange("(u p e) c -> p u e c", u=HALVES, e=2)
        res_view = w_res.rearrange("(p h i) d -> p h i d", h=2, i=2)

        def load_taps(name, view):
            return [load("%s_%d" % (name, e), [P, TAPS * CH], view[:, e, :]) for e in range(2)]

        sig_rows = [None] * HALVES
        gate_rows = [None] * HALVES
        psig_rows = [None] * HALVES
        pgate_rows = [None] * HALVES
        psig_rows[0] = load("psig0", [P, 2, CH], psig_view[:, 0])
        sig_rows[0] = load_taps("sig0", sig_view[:, 0])
        x_sb = load("x_sb", [P, B * PACK, T], x.rearrange("b (j p) t -> p (b j) t", p=P))
        pgate_rows[0] = load("pgate0", [P, 2, CH], pgate_view[:, 0])
        for g, b_vec in enumerate((b_sig, b_gate)):
            nc.sync.dma_start(
                out=bias_rows[g * HALVES : (g + 1) * HALVES, :].bitcast(BF16),
                in_=b_vec.rearrange("(u w) -> u w", u=HALVES),
            )
        gate_rows[0] = load_taps("gate0", gate_view[:, 0])
        c_sb = load(
            "c_sb", [P, B * HALVES, 2 * T], cond.rearrange("b (u p e) t -> p (b u) (e t)", u=HALVES, e=2)
        )
        sig_rows[1] = load_taps("sig1", sig_view[:, 1])
        psig_rows[1] = load("psig1", [P, 2, CH], psig_view[:, 1])
        gate_rows[1] = load_taps("gate1", gate_view[:, 1])
        pgate_rows[1] = load("pgate1", [P, 2, CH], pgate_view[:, 1])
        res_rows = [load("res%d" % h, [P, 2, CH], res_view[:, h]) for h in range(2)]
        skp_rows = load("skp", [P, 1, CH], w_skp.rearrange("s (o d) -> s o d", o=1))
        x_res = load("x_res", [P, B, PACK * T], x.rearrange("b (p j) t -> p b (j t)", j=PACK))

        def quantise(name, grouped_flat, columns):
            codes = mx.tile([P, columns], U32, name=name + "_codes", align_bytes=64)
            scales = mx.tile([P, columns], U8, name=name + "_scales", align_bytes=64)
            nc.vector.quantize_mx(out=codes[:].bitcast(FP8X4), scales=scales[:], in_=grouped_flat)
            return codes, scales

        def turn_taps(name, rows, empty_banks):
            flat = []
            for e in range(2):
                words = rows[e][:].bitcast(F32)
                bank = turned.tile([P, PACK, P], F32, tag="bank", name="%s%d_bank" % (name, e))
                for j in range(PACK):
                    nc.tensor.transpose(bank[:, j, :], words[:, j * P : (j + 1) * P], ident[:])
                grouped = stage.tile([P, TAPS, P, PACK], BF16, name="%s%d_grouped" % (name, e), align_bytes=64)
                empty_banks[e](out=grouped[:], in_=bank[:].bitcast(BF16).rearrange("p j (m t) -> p t m j", t=TAPS))
                flat.append(grouped[:].rearrange("p t m j -> p (t m j)"))
            return flat

        def turn_plain(name, rows, chunks, empty_bank):
            bank = turned.tile([P, chunks, HALVES, P], F32, tag="bank", name=name + "_bank")
            for i in range(chunks):
                words = rows[:, i, :].bitcast(F32)
                for v in range(HALVES):
                    nc.tensor.transpose(bank[:, i, v, :], words[:, v * P : (v + 1) * P], ident[:])
            grouped = stage.tile([P, chunks, P, PACK], BF16, name=name + "_grouped", align_bytes=64)
            empty_bank(out=grouped[:].bitcast(F32), in_=bank[:].rearrange("p i v m -> p i m v"))
            return grouped[:].rearrange("p i m t -> p (i m t)")

        def mx_pass(out, weights, first, moving, moving_first, start, stop, columns=N):
            w_codes, w_scales = weights
            m_codes, m_scales = moving
            nc.tensor.matmul_mx(
                out=out,
                lhsT=w_codes[:, first : first + P].bitcast(FP8X4),
                lhsT_scale=w_scales[:, first : first + P],
                rhs=m_codes[:, moving_first : moving_first + columns].bitcast(FP8X4),
                rhs_scale=m_scales[:, moving_first : moving_first + columns],
                start=start,
                stop=stop,
            )

        def keep_clock_mx(times, spare_sum):
            for i in range(times):
                mx_pass(spare_sum[:], x_mx, 0, x_mx, 0, True, True, TAPS * N)

        tanh_filt = stage.tile([P, PACK, N], F32)
        sigm_gate = stage.tile([P, PACK, N], F32)

        def gate_acts(g, u, accs):
            for e in range(2):
                s = 2 * u + e
                nc.scalar.activation(
                    out=(tanh_filt, sigm_gate)[g][:, s, :],
                    in_=accs[e],
                    func=(ACT.Tanh, ACT.Sigmoid)[g],
                    bias=bias[:, g, s : s + 1],
                )

        def branch(g, u, taps_mx, proj_mx):
            acc = sums.tile([P, 2, N], F32, tag="sum", name="acc%d%d" % (g, u))
            for e in range(2):
                mx_pass(acc[:, e, :], taps_mx[e], 0, x_mx, 0, True, False)
                mx_pass(acc[:, e, :], taps_mx[e], P, x_mx, N, False, False)
                mx_pass(acc[:, e, :], proj_mx, e * P, c_mx, 0, False, True)
            gate_acts(g, u, [acc[:, e, :] for e in range(2)])

        by_scalar = nc.scalar.copy
        by_vector = nc.vector.tensor_copy

        psig_g = turn_plain("psig0", psig_rows[0], 2, by_scalar)
        keep_clock(1)
        psig0_mx = quantise("psig0", psig_g, 2 * P)
        sig_g = turn_taps("sig0", sig_rows[0], (by_scalar, by_scalar))
        keep_clock(3)
        x_grouped = stage.tile([P, TAPS, B, DIL, PACK], BF16, align_bytes=64)
        x_by_time = x_sb[:].rearrange("p (b j) t -> p b t j", b=B)
        for tap in range(TAPS):
            nc.vector.tensor_copy(out=x_grouped[:, tap], in_=x_by_time[:, :, tap * DIL : (tap + 1) * DIL])
        sig0_mx = [quantise("sig00", sig_g[0], TAPS * P)]
        x_mx = quantise("x", x_grouped[:].rearrange("p h b t j -> p (h b t j)"), TAPS * N)
        sig0_mx.append(quantise("sig01", sig_g[1], TAPS * P))

        pgate_g = turn_plain("pgate0", pgate_rows[0], 2, by_vector)
        bias_bank = turned.tile([P, P], F32, tag="bank")
        nc.tensor.transpose(bias_bank[:], bias_rows[:], ident[:])
        keep_clock(1)
        bias = const.tile([P, 2, PACK], BF16)
        nc.vector.tensor_copy(
            out=bias[:].rearrange("p g s -> p (g s)").bitcast(F32), in_=bias_bank[:, 0 : 2 * HALVES]
        )

        gate_g = turn_taps("gate0", gate_rows[0], (by_scalar, by_scalar))
        keep_clock(1)
        keep_clock_mx(3, spare)
        c_grouped = stage.tile([P, B, DIL, PACK], BF16, align_bytes=64)
        c_by_time = c_sb[:].rearrange("p (b u) (e t) -> p b t (u e)", b=B, e=2)
        nc.vector.tensor_copy(out=c_grouped[:], in_=c_by_time[:, :, DIL:T, :])
        pgate0_mx = quantise("pgate0", pgate_g, 2 * P)
        gate0_mx = [quantise("gate00", gate_g[0], TAPS * P)]
        c_mx = quantise("c", c_grouped[:].rearrange("p b t s -> p (b t s)"), N)
        gate0_mx.append(quantise("gate01", gate_g[1], TAPS * P))

        sig_g = turn_taps("sig1", sig_rows[1], (by_scalar, by_vector))
        keep_clock(1)
        psig_g = turn_plain("psig1", psig_rows[1], 2, by_scalar)
        branch(0, 0, sig0_mx, psig0_mx)
        sig1_mx = [quantise("sig10", sig_g[0], 2 * P)]
        psig1_mx = quantise("psig1", psig_g, 2 * P)
        sig1_mx.append(quantise("sig11", sig_g[1], 2 * P))

        gate_g = turn_taps("gate1", gate_rows[1], (by_scalar, by_vector))
        pgate_g = turn_plain("pgate1", pgate_rows[1], 2, by_scalar)
        branch(1, 0, gate0_mx, pgate0_mx)
        branch(0, 1, sig1_mx, psig1_mx)
        gate1_mx = [quantise("gate1%d" % e, gate_g[e], TAPS * P) for e in range(2)]
        pgate1_mx = quantise("pgate1", pgate_g, 2 * P)

        res_g = [turn_plain("res%d" % h, res_rows[h], 2, (by_vector, by_scalar)[h]) for h in range(2)]

        accs = [sums.tile([P, N], F32, tag="sum", name="acc11%d" % e) for e in range(2)]
        for e in range(2):
            for t in range(TAPS):
                mx_pass(accs[e][:], gate1_mx[e], t * P, x_mx, t * N, t == 0, False)
        for e in range(2):
            mx_pass(accs[e][:], pgate1_mx, e * P, c_mx, 0, False, True)
        gate_acts(1, 1, [accs[e][:] for e in range(2)])

        skp_g = turn_plain("skp", skp_rows, 1, by_scalar)
        keep_clock_mx(4, sums.tile([P, TAPS * N], F32, tag="sum", name="spare_late"))
        res_mx = [None, quantise("res1", res_g[1], 2 * P)]

        z_grouped = stage.tile([P, N, PACK], BF16, align_bytes=64)
        nc.vector.tensor_tensor(
            out=z_grouped[:],
            in0=tanh_filt[:].rearrange("p s n -> p n s"),
            in1=sigm_gate[:].rearrange("p s n -> p n s"),
            op=ALU.mult,
        )
        res_mx[0] = quantise("res0", res_g[0], 2 * P)
        z_mx = quantise("z", z_grouped[:].rearrange("p n s -> p (n s)"), N)
        skp_mx = quantise("skp", skp_g, P)

        res_sum = sums.tile([P, PACK, B, DIL], F32, tag="sum")
        for j in range(PACK):
            mx_pass(res_sum[:, j].rearrange("p b t -> p (b t)"), res_mx[j // 2], (j % 2) * P, z_mx, 0, True, True)
        skp_sum = sums.tile([P, N], F32, tag="sum")
        mx_pass(skp_sum[:], skp_mx, 0, z_mx, 0, True, True)

        skp_sb = stage.tile([P, B, DIL], F32)
        nc.scalar.copy(out=skp_sb[:].rearrange("p b t -> p (b t)"), in_=skp_sum[:])
        nc.sync.dma_start(out=out_1.rearrange("b s t -> s b t"), in_=skp_sb[:])

        x_later = x_res[:].rearrange("p b (j t) -> p b j t", j=PACK)[:, :, :, DIL:T]
        sig_sb = stage.tile([P, B, PACK, DIL], F32)
        for b in range(B):
            nc.vector.tensor_tensor(out=sig_sb[:, b], in0=res_sum[:, :, b, :], in1=x_later[:, b], op=ALU.add)
            nc.sync.dma_start(
                out=out_0[b].rearrange("(p j) t -> p (j t)", j=PACK), in_=sig_sb[:, b].rearrange("p j t -> p (j t)")
            )
